import numpy as np
import ml_dtypes


def mxq(x, axis, fmt="e4m3"):
    dtype, down = {"e4m3": (ml_dtypes.float8_e4m3fn, 7), "e5m2": (ml_dtypes.float8_e5m2, 14)}[fmt]
    v = np.moveaxis(np.asarray(x, np.float32).astype(ml_dtypes.bfloat16).astype(np.float64), axis, -1)
    blocks = v.reshape(v.shape[:-1] + (-1, 32))
    amax = np.abs(blocks).max(-1, keepdims=True)
    byte = np.maximum(np.where(amax > 0, np.frexp(amax)[1] - 1 + 127, 0) - down, 1)
    scale = np.exp2(byte - 127.0)
    codes = (blocks / scale).astype(np.float32).astype(dtype).astype(np.float64)
    return np.moveaxis((codes * scale).reshape(v.shape), -1, axis)


WIDE = False


def mx_kscale(k):
    if not WIDE:
        return np.ones(k)
    levels = np.array([18, -18])
    if k % 512:
        return np.exp2(np.random.permutation(np.resize(levels, k // 32))).repeat(32)
    a = np.empty((k // 512, 16))
    for p in range(k // 512):
        a[p, :8] = np.random.permutation(np.resize(levels, 8))
        for g in range(8):
            far = levels[np.abs(levels - a[p, g]) >= 10]
            a[p, g + 8] = far[np.random.randint(len(far))]
    return np.exp2(a.ravel()).repeat(32)


BF16 = ml_dtypes.bfloat16


def bf(x):
    return np.asarray(x, np.float32).astype(BF16)


def f64(x):
    return np.asarray(x).astype(np.float64)


B, CIN, H, W, COUT, SP, K = 16, 1024, 8, 8, 1024, 8, 7
PAD = K // 2
KK = K * K
HN = COUT // SP
HW = H * W
T = B * HW
OFFS = [(dy, dx) for dy in range(K) for dx in range(K)]


def logsumexp(lg):
    m = lg.max(axis=2, keepdims=True)
    return (m + np.log(np.exp(lg - m).sum(axis=2, keepdims=True)))[:, :, 0]


def fold(dp, axis, n):
    v = np.moveaxis(dp, axis, 0)
    core = v[PAD:PAD + n].copy()
    core[1:PAD + 1] += v[:PAD][::-1]
    core[n - 1 - PAD:n - 1] += v[PAD + n:][::-1]
    return np.moveaxis(core, 0, axis)


def setup_inputs():
    s = mx_kscale(T)[::HW][:, None, None, None]
    u = mx_kscale(COUT)
    logits = bf(np.random.standard_normal((B, HN, KK, HW)) * 1.5)
    x0 = bf(np.random.standard_normal((B, CIN, H, W)))
    w0 = bf(np.random.standard_normal((COUT, CIN)) * 2.0 / np.sqrt(CIN))
    b3c = bf(np.random.standard_normal(COUT) * 0.5)
    g = bf(np.random.standard_normal((B, COUT, H, W)) * np.exp2(np.random.randint(-6, 1, (B, 1, H, W)))
           / s * u[None, :, None, None])
    lse = logsumexp(f64(logits))
    return {
        "logits": logits,
        "x": bf(f64(x0) * s),
        "w3c": bf(f64(w0) / u[:, None]),
        "b3c": b3c,
        "lse": np.asarray(lse, np.float32),
        "grad_out": g,
    }


def reference(logits, x, w3c, b3c, lse, grad_out):
    wgt = np.exp(f64(logits) - f64(lse)[:, :, None, :]).reshape(B, HN, KK, H, W)
    g = f64(grad_out).reshape(B, HN, SP, H, W)
    dp = np.zeros((B, HN, SP, H + 2 * PAD, W + 2 * PAD))
    for k, (dy, dx) in enumerate(OFFS):
        dp[:, :, :, dy:dy + H, dx:dx + W] += g * wgt[:, :, k][:, :, None]
    d3 = fold(fold(dp, 3, H), 4, W)
    dz = d3.reshape(B, COUT, HW).transpose(1, 0, 2).reshape(COUT, T)
    xt = f64(x).reshape(B, CIN, HW).transpose(1, 0, 2).reshape(CIN, T)
    gx = mxq(f64(w3c), 0, "e4m3").T @ mxq(dz, 0, "e5m2")
    gw = mxq(dz, 1, "e5m2") @ mxq(xt, 1, "e4m3").T
    gx = gx.reshape(CIN, B, HW).transpose(1, 0, 2).reshape(B, CIN, H, W)
    return gx, gw

@@ -1,0 +1,318 @@
+from contextlib import ExitStack
+
+import concourse.mybir as mybir
+from concourse.masks import make_identity
+
+F32 = mybir.dt.float32
+BF16 = mybir.dt.bfloat16
+U32 = mybir.dt.uint32
+U8 = mybir.dt.uint8
+E4X4 = mybir.dt.float8_e4m3fn_x4
+E5X4 = mybir.dt.float8_e5m2_x4
+ADD = mybir.AluOpType.add
+SUB = mybir.AluOpType.subtract
+MUL = mybir.AluOpType.mult
+EXP = mybir.ActivationFunctionType.Exp
+COPY = mybir.ActivationFunctionType.Copy
+AX = mybir.AxisListType.X
+
+FLOPS = 2 * 2 * 1024 * 1024 * 1024 + 2 * 49 * 1024 * 1024
+
+PITCH = 129
+BASE = 36 * PITCH
+PLEN = 16384
+
+
+def tile_sam_pb_v_kernel(tc, logits, x, w3c, b3c, lse, grad_out, out_0, out_1):
+    nc = tc.nc
+    with ExitStack() as ctx:
+        keep = ctx.enter_context(tc.tile_pool(name="keep", bufs=1))
+        identf = keep.tile([128, 128], F32, name="identf")
+        make_identity(nc, identf[:])
+        identb = keep.tile([128, 128], BF16, name="identb")
+        make_identity(nc, identb[:])
+        par = keep.tile([128, 2], F32, name="par")
+        nc.vector.tensor_reduce(par[:], identf[:].rearrange("p (n e) -> p e n", e=2), axis=AX, op=ADD)
+
+        qf = [keep.tile([128, 1024, 4], BF16, name="qf%d" % g, align_bytes=64) for g in range(2)]
+        wc = [keep.tile([128, 1024], U32, name="wc%d" % g, align_bytes=64) for g in range(2)]
+        ws = [keep.tile([128, 1024], U8, name="ws%d" % g, align_bytes=64) for g in range(2)]
+        xc = [keep.tile([128, 1024], U32, name="xc%d" % g, align_bytes=64) for g in range(2)]
+        xs = [keep.tile([128, 1024], U8, name="xs%d" % g, align_bytes=64) for g in range(2)]
+
+        with ExitStack() as mctx:
+            big = mctx.enter_context(tc.tile_pool(name="big", bufs=1))
+            pool = mctx.enter_context(tc.tile_pool(name="pool", bufs=2))
+            psT = mctx.enter_context(tc.psum_pool(name="psT", bufs=4))
+            psM = mctx.enter_context(tc.psum_pool(name="psM", bufs=2))
+            psA = mctx.enter_context(tc.psum_pool(name="psA", bufs=2))
+
+            lset = big.tile([128, 16, 64], F32, name="lset")
+            nc.sync.dma_start(out=lset[:], in_=lse.rearrange("b h n -> h b n"))
+            P = big.tile([128, PLEN], F32, name="P")
+            nc.gpsimd.memset(P[:], 0.0)
+            Pv = P[:, BASE:BASE + 56 * PITCH].rearrange("p (x y w) -> p x y w", x=7, y=8)
+            D = big.tile([128, 2, 7, 7, 8, 8], F32, name="D")
+
+            lgs = {}
+            gls = {}
+
+            def load_logits(n):
+                if n < 16:
+                    t = pool.tile([128, 49, 64], BF16, name="lg", bufs=3)
+                    nc.sync.dma_start(out=t[:], in_=logits[n])
+                    lgs[n] = t
+
+            def load_grad(q):
+                if q < 8:
+                    t = pool.tile([128, 2, 8, 8, 8], BF16, name="gl", bufs=2)
+                    for im in range(2):
+                        nc.sync.dma_start(
+                            out=t[:, im].rearrange("p c i j -> p (c i j)"),
+                            in_=grad_out[2 * q + im].rearrange("(h c) i j -> h (c i j)", c=8))
+                    gls[q] = t
+
+            def expo(q, im):
+                n = 2 * q + im
+                dv = D[:, im].rearrange("p y x i j -> p (y x) (i j)")
+                nc.vector.tensor_tensor(
+                    out=dv, in0=lgs[n][:],
+                    in1=lset[:, n:n + 1, :].to_broadcast([128, 49, 64]), op=SUB)
+                nc.scalar.activation(out=dv, in_=dv, func=EXP)
+                load_logits(n + 3)
+
+            def rowfold(q, im):
+                for i in (0, 1, 2, 5, 6, 7):
+                    A = D[:, im, :, :, i, :]
+                    if i < 3:
+                        dst, src, dead = slice(4 - i, 7 - 2 * i), slice(2 - i, None, -1), slice(0, 3 - i)
+                    else:
+                        dst, src, dead = slice(14 - 2 * i, 10 - i), slice(6, 10 - i, -1), slice(11 - i, 7)
+                    nc.vector.tensor_tensor(out=A[:, dst], in0=A[:, dst], in1=A[:, src], op=ADD)
+                    nc.gpsimd.memset(A[:, dead], 0.0)
+
+            def place(q):
+                for im in (1, 0):
+                    dst = Pv[:, :, 0:7, 65 * im:65 * im + 64].rearrange("p x y (j i) -> p x y j i", i=8)
+                    src = D[:, im, ::-1, ::-1].rearrange("p y x i j -> p x y j i")
+                    if im == 0:
+                        nc.vector.tensor_copy(out=dst, in_=src)
+                    else:
+                        nc.scalar.copy(out=dst, in_=src)
+                for im in range(2):
+                    for j in (0, 1, 2, 5, 6, 7):
+                        A = Pv[:, :, 0:7, 65 * im + 8 * j:65 * im + 8 * j + 8]
+                        if j < 3:
+                            ds, ss = slice(2 * j, j + 3), slice(6, 3 + j, -1)
+                        else:
+                            ds, ss = slice(j - 3, 2 * j - 7), slice(j - 5, None, -1)
+                        nc.vector.tensor_tensor(out=A[:, ds], in0=A[:, ds], in1=A[:, ss], op=ADD)
+
+            gms = {}
+
+            def gprep(q):
+                gl = gls[q]
+                gr = pool.tile([128, 4, 2, 8, 8, 2], BF16, name="gr", bufs=1)
+                for cl in range(4):
+                    nc.vector.tensor_copy(
+                        out=gr[:, cl],
+                        in_=gl[:].rearrange("p m (a b) i j -> p b a j i m", b=4)[:, cl])
+                gt = psA.tile([128, 8, 128], BF16, name="aux")
+                grv = gr[:].rearrange("p b a j i m -> p (b a) (j i m)")
+                for c in range(8):
+                    nc.tensor.transpose(gt[:, c, :], grv[:, c, :], identb[:])
+                gx = pool.tile([128, 64, 2, 8], BF16, name="gx", bufs=2)
+                for im in range(2):
+                    nc.scalar.activation(
+                        out=gx[:, :, im, :], in_=gt[:, :, 0:64].rearrange("p c r -> p r c"),
+                        func=COPY, scale=par[:, im:im + 1])
+                gy = pool.tile([128, 64, 8], F32, name="gy", bufs=2)
+                nc.vector.tensor_copy(out=gy[:], in_=gt[:, :, 64:128].rearrange("p c r -> p r c"))
+                gms[q] = (gx, gy)
+
+            wms = {}
+
+            def tstage(q, extra):
+                wx = pool.tile([128, 2, 64, 64], BF16, name="wx", bufs=1)
+                wy = pool.tile([128, 64, 128], F32, name="wy", bufs=1)
+                for k in range(16):
+                    tb = psT.tile([128, 4, 128], F32, name="tb")
+                    for a in range(4):
+                        i, j = divmod(4 * k + a, 8)
+                        s = BASE + PITCH * (27 - (8 * j + i))
+                        nc.tensor.transpose(tb[:, a, :], P[:, s:s + 65 * 127 + 1:65], identf[:])
+                    hi = wx[:, 0, 4 * k:4 * k + 4, :]
+                    lo = wx[:, 1, 4 * k:4 * k + 4, :]
+                    nc.scalar.copy(out=hi, in_=tb[:, :, 0:64])
+                    tv = tb[:, :, 64:128].rearrange("p a r -> p r a")
+                    nc.scalar.activation(out=wy[:, :, 4 * k:4 * k + 4], in_=tv, func=COPY, scale=par[:, 0:1])
+                    nc.vector.tensor_tensor(out=lo, in0=tb[:, :, 0:64], in1=hi, op=SUB)
+                    nc.vector.tensor_scalar(out=wy[:, :, 64 + 4 * k:64 + 4 * k + 4], in0=tv,
+                                            scalar1=par[:, 1:2], scalar2=None, op0=MUL)
+                    for f in extra.get(k, ()):
+                        f()
+                wms[q] = (wx, wy)
+
+            dzs = {}
+
+            def mstage(q):
+                gx, gy = gms[q]
+                wx, wy = wms[q]
+                wxv = wx[:].rearrange("p a n r -> p (a n) r")
+                dzx = pool.tile([128, 8, 128], F32, name="dzx", bufs=1)
+                for s in range(2):
+                    mb = psM.tile([128, 8, 64], F32, name="mb")
+                    for r in range(32):
+                        nc.tensor.matmul(
+                            mb[:, :, 2 * r:2 * r + 2], lhsT=wxv[:, :, 32 * s + r],
+                            rhs=gx[:, 32 * s + r].rearrange("p m c -> p (m c)"), start=True, stop=True)
+                    nc.scalar.copy(out=dzx[:, :, 64 * s:64 * s + 64], in_=mb[:])
+                    if q + 2 < 8:
+                        expo(q + 2, s)
+                dzy = pool.tile([128, 4, 128], F32, name="dzy", bufs=1)
+                mb = psM.tile([128, 4, 128], F32, name="mb")
+                for r in range(64):
+                    nc.tensor.matmul(mb[:, :, 2 * r:2 * r + 2], lhsT=wy[:, r, :], rhs=gy[:, r, :],
+                                     start=True, stop=True)
+                nc.scalar.copy(out=dzy[:], in_=mb[:])
+                dzs[q] = (dzx, dzy)
+
+            def dz_split(q, im):
+                dzx, dzy = dzs[q]
+                zb = psA.tile([128, 4, 128], F32, name="aux")
+                for t in range(4):
+                    nc.tensor.transpose(zb[:, t, :], dzx[:, 4 * im + t, :], identf[:])
+                k0 = 128 * q + 64 * im
+                with nc.allow_low_precision(reason="dz is rounded once to bfloat16"):
+                    nc.vector.tensor_reduce(
+                        qf[0][:, k0:k0 + 64, :],
+                        zb[:].rearrange("p t (a n) -> p n t a", a=2), axis=AX, op=ADD)
+
+            def dz_whole(q):
+                dzx, dzy = dzs[q]
+                zb = psA.tile([128, 4, 128], F32, name="aux")
+                for t in range(4):
+                    nc.tensor.transpose(zb[:, t, :], dzy[:, t, :], identf[:])
+                nc.scalar.copy(out=qf[1][:, 128 * q:128 * q + 128, :], in_=zb[:].rearrange("p t n -> p n t"))
+
+            def wprep(q):
+                g, cq = divmod(q, 4)
+                wl = pool.tile([128, 4, 256], BF16, name="wl", bufs=1)
+                cols = slice(256 * cq, 256 * cq + 256)
+                nc.sync.dma_start(
+                    out=wl[:], in_=w3c.rearrange("(g p j) w -> g p j w", g=2, j=4)[g][:, :, cols])
+                wi = pool.tile([128, 256, 4], BF16, name="wi", bufs=1, align_bytes=64)
+                nc.vector.tensor_copy(out=wi[:], in_=wl[:].rearrange("p j w -> p w j"))
+                nc.vector.quantize_mx(out=wc[g][:, cols].bitcast(E4X4), scales=ws[g][:, cols],
+                                      in_=wi[:].rearrange("p w j -> p (w j)"))
+
+            def xprep(q):
+                xi = pool.tile([128, 2, 128, 4], BF16, name="xi", bufs=1, align_bytes=64)
+                xl = pool.tile([128, 16, 64], BF16, name="xl", bufs=2)
+                nc.sync.dma_start(
+                    out=xl[:], in_=x.rearrange("b (k c) i j -> k c b (i j)", c=128)[q])
+                xw = xl[:].rearrange("p b n -> p (b n)").bitcast(F32)
+                xb = psA.tile([128, 4, 128], F32, name="aux")
+                for hv in range(4):
+                    h, v = divmod(hv, 2)
+                    nc.tensor.transpose(xb[:, hv, :], xw[:, 256 * h + v:256 * h + 256:2], identf[:])
+                for h in range(2):
+                    nc.scalar.copy(
+                        out=xi[:, h].rearrange("p c u -> p (c u)").bitcast(F32).rearrange("p (c v) -> p c v", v=2),
+                        in_=xb[:, 2 * h:2 * h + 2, :].rearrange("p v c -> p c v"))
+                    cols = slice(128 * q, 128 * q + 128)
+                    nc.vector.quantize_mx(out=xc[h][:, cols].bitcast(E4X4), scales=xs[h][:, cols],
+                                          in_=xi[:, h].rearrange("p c u -> p (c u)"))
+
+            for n in range(3):
+                load_logits(n)
+            load_grad(0)
+            with tc.manual_schedule():
+                for im in range(2):
+                    expo(0, im)
+                    rowfold(0, im)
+                place(0)
+                for im in range(2):
+                    expo(1, im)
+                for q in range(8):
+                    load_grad(q + 1)
+                    extra = {k: [] for k in range(16)}
+                    extra[9].append(lambda: gprep(q))
+                    if q > 0:
+                        extra[1].append(lambda: dz_split(q - 1, 0))
+                        extra[3].append(lambda: dz_split(q - 1, 1))
+                        extra[5].append(lambda: dz_whole(q - 1))
+                    if q < 7:
+                        extra[4].append(lambda: rowfold(q + 1, 0))
+                        extra[7].append(lambda: rowfold(q + 1, 1))
+                    extra[11].append(lambda: wprep(q))
+                    extra[13].append(lambda: xprep(q))
+                    tstage(q, extra)
+                    if q < 7:
+                        place(q + 1)
+                    mstage(q)
+                for im in range(2):
+                    dz_split(7, im)
+                dz_whole(7)
+
+        with ExitStack() as ectx:
+            fin = ectx.enter_context(tc.tile_pool(name="fin", bufs=2))
+            ps = ectx.enter_context(tc.psum_pool(name="ps", bufs=4))
+            qc = [[fin.tile([128, 512], U32, name="qc%d%d" % (g, h), align_bytes=64, bufs=1) for h in range(2)] for g in range(2)]
+            qs = [[fin.tile([128, 512], U8, name="qs%d%d" % (g, h), align_bytes=64, bufs=1) for h in range(2)] for g in range(2)]
+            tcod = [fin.tile([128, 1024], U32, name="tc%d" % h, align_bytes=64, bufs=1) for h in range(2)]
+            tsc = [fin.tile([128, 1024], U8, name="ts%d" % h, align_bytes=64, bufs=1) for h in range(2)]
+            turn = 0
+            for h in range(2):
+                for g in range(2):
+                    nc.vector.quantize_mx(
+                        out=qc[g][h][:].bitcast(E5X4), scales=qs[g][h][:],
+                        in_=qf[g][:, 512 * h:512 * h + 512, :].rearrange("p k t -> p (k t)"))
+                    qt = fin.tile([128, 4, 128, 4], BF16, name="qt", align_bytes=64)
+                    for t in range(4):
+                        tb = ps.tile([128, 4, 128], BF16, name="tt")
+                        for u in range(4):
+                            nc.tensor.transpose(tb[:, u, :], qf[g][:, 512 * h + u:512 * h + 512:4, t], identb[:])
+                        if t % 2 == 0:
+                            nc.vector.tensor_copy(out=qt[:, t], in_=tb[:].rearrange("p u o -> p o u"))
+                        else:
+                            nc.scalar.copy(out=qt[:, t], in_=tb[:].rearrange("p u o -> p o u"))
+                    cols = slice(512 * g, 512 * g + 512)
+                    nc.vector.quantize_mx(out=tcod[h][:, cols].bitcast(E5X4), scales=tsc[h][:, cols],
+                                          in_=qt[:].rearrange("p t o u -> p (t o u)"))
+
+            o0 = out_0.rearrange("b (k c) i j -> k c b (i j)", c=128)
+            o1 = out_1.rearrange("(g p t) w -> g t p w", g=2, t=4)
+
+            def emit(acc, dst, shape_b):
+                st = fin.tile([128, 512], F32, name="st", bufs=6)
+                if emitted[0] % 2 == 0:
+                    nc.vector.tensor_copy(out=st[:], in_=acc[:])
+                else:
+                    nc.scalar.copy(out=st[:], in_=acc[:])
+                emitted[0] += 1
+                if shape_b:
+                    nc.sync.dma_start(out=dst, in_=st[:].rearrange("p (b n) -> p b n", n=64))
+                else:
+                    nc.sync.dma_start(out=dst, in_=st[:])
+
+            emitted = [0]
+            for h in range(2):
+                for k in range(8):
+                    acc = ps.tile([128, 512], F32, name="acc")
+                    for g in range(2):
+                        nc.tensor.matmul_mx(
+                            out=acc[:], lhsT=wc[g][:, 128 * k:128 * k + 128].bitcast(E4X4),
+                            lhsT_scale=ws[g][:, 128 * k:128 * k + 128],
+                            rhs=qc[g][h][:].bitcast(E5X4), rhs_scale=qs[g][h][:], start=(g == 0), stop=(g == 1))
+                    emit(acc, o0[k][:, 8 * h:8 * h + 8, :], True)
+            for gt in range(8):
+                for ch in range(2):
+                    acc = ps.tile([128, 512], F32, name="acc")
+                    for h in range(2):
+                        nc.tensor.matmul_mx(
+                            out=acc[:], lhsT=tcod[h][:, 128 * gt:128 * gt + 128].bitcast(E5X4),
+                            lhsT_scale=tsc[h][:, 128 * gt:128 * gt + 128],
+                            rhs=xc[h][:, 512 * ch:512 * ch + 512].bitcast(E4X4),
+                            rhs_scale=xs[h][:, 512 * ch:512 * ch + 512], start=(h == 0), stop=(h == 1))
+                    emit(acc, o1[gt // 4][gt % 4][:, 512 * ch:512 * ch + 512], False)

@@ -21,6 +21,9 @@ FLOPS = 2 * 2 * 1024 * 1024 * 1024 + 2 * 49 * 1024 * 1024
 PITCH = 129
 BASE = 36 * PITCH
 PLEN = 16384
+XG = 6
+NZT = 3
+NZM = 5
 
 
 def tile_sam_pb_v_kernel(tc, logits, x, w3c, b3c, lse, grad_out, out_0, out_1):
@@ -48,23 +51,32 @@ def tile_sam_pb_v_kernel(tc, logits, x, w3c, b3c, lse, grad_out, out_0, out_1):
             psA = mctx.enter_context(tc.psum_pool(name="psA", bufs=2))
 
             lset = big.tile([128, 16, 64], F32, name="lset")
-            nc.sync.dma_start(out=lset[:], in_=lse.rearrange("b h n -> h b n"))
             P = big.tile([128, PLEN], F32, name="P")
-            nc.gpsimd.memset(P[:], 0.0)
             Pv = P[:, BASE:BASE + 56 * PITCH].rearrange("p (x y w) -> p x y w", x=7, y=8)
             D = big.tile([128, 2, 7, 7, 8, 8], F32, name="D")
+            Dz = big.tile([128, 7, 7, 8, 8], F32, name="Dz")
 
             lgs = {}
             gls = {}
+            gzs = {}
+            order = [0, 1, 12, 2, 3, 4, 5, 13, 6, 7, 8, 9, 14, 10, 11, 15]
+            loaded = [0]
 
-            def load_logits(n):
-                if n < 16:
+            def load_logits():
+                if loaded[0] < 16:
+                    n = order[loaded[0]]
+                    loaded[0] += 1
                     t = pool.tile([128, 49, 64], BF16, name="lg", bufs=3)
                     nc.sync.dma_start(out=t[:], in_=logits[n])
                     lgs[n] = t
+                    if n >= 12:
+                        t = pool.tile([128, 8, 8, 8], BF16, name="gz", bufs=2)
+                        nc.sync.dma_start(out=t[:].rearrange("p c i j -> p (c i j)"),
+                                          in_=grad_out[n].rearrange("(h c) i j -> h (c i j)", c=8))
+                        gzs[n] = t
 
             def load_grad(q):
-                if q < 8:
+                if q < XG:
                     t = pool.tile([128, 2, 8, 8, 8], BF16, name="gl", bufs=2)
                     for im in range(2):
                         nc.sync.dma_start(
@@ -72,41 +84,115 @@ def tile_sam_pb_v_kernel(tc, logits, x, w3c, b3c, lse, grad_out, out_0, out_1):
                             in_=grad_out[2 * q + im].rearrange("(h c) i j -> h (c i j)", c=8))
                     gls[q] = t
 
-            def expo(q, im):
-                n = 2 * q + im
-                dv = D[:, im].rearrange("p y x i j -> p (y x) (i j)")
+            def expo(n, dst):
+                dv = dst.rearrange("p y x i j -> p (y x) (i j)")
                 nc.vector.tensor_tensor(
                     out=dv, in0=lgs[n][:],
                     in1=lset[:, n:n + 1, :].to_broadcast([128, 49, 64]), op=SUB)
                 nc.scalar.activation(out=dv, in_=dv, func=EXP)
-                load_logits(n + 3)
+                load_logits()
 
-            def rowfold(q, im):
+            def rowfold(dst, clear):
                 for i in (0, 1, 2, 5, 6, 7):
-                    A = D[:, im, :, :, i, :]
+                    A = dst[:, :, :, i, :]
                     if i < 3:
-                        dst, src, dead = slice(4 - i, 7 - 2 * i), slice(2 - i, None, -1), slice(0, 3 - i)
+                        ds, ss, dead = slice(4 - i, 7 - 2 * i), slice(2 - i, None, -1), slice(0, 3 - i)
                     else:
-                        dst, src, dead = slice(14 - 2 * i, 10 - i), slice(6, 10 - i, -1), slice(11 - i, 7)
-                    nc.vector.tensor_tensor(out=A[:, dst], in0=A[:, dst], in1=A[:, src], op=ADD)
-                    nc.gpsimd.memset(A[:, dead], 0.0)
+                        ds, ss, dead = slice(14 - 2 * i, 10 - i), slice(6, 10 - i, -1), slice(11 - i, 7)
+                    nc.vector.tensor_tensor(out=A[:, ds], in0=A[:, ds], in1=A[:, ss], op=ADD)
+                    if clear:
+                        nc.gpsimd.memset(A[:, dead], 0.0)
 
-            def place(q):
-                for im in (1, 0):
-                    dst = Pv[:, :, 0:7, 65 * im:65 * im + 64].rearrange("p x y (j i) -> p x y j i", i=8)
-                    src = D[:, im, ::-1, ::-1].rearrange("p y x i j -> p x y j i")
-                    if im == 0:
-                        nc.vector.tensor_copy(out=dst, in_=src)
+            def colfold(rows):
+                for j in (0, 1, 2, 5, 6, 7):
+                    A = rows(j)
+                    if j < 3:
+                        ds, ss = slice(2 * j, j + 3), slice(6, 3 + j, -1)
                     else:
-                        nc.scalar.copy(out=dst, in_=src)
-                for im in range(2):
-                    for j in (0, 1, 2, 5, 6, 7):
-                        A = Pv[:, :, 0:7, 65 * im + 8 * j:65 * im + 8 * j + 8]
-                        if j < 3:
-                            ds, ss = slice(2 * j, j + 3), slice(6, 3 + j, -1)
-                        else:
-                            ds, ss = slice(j - 3, 2 * j - 7), slice(j - 5, None, -1)
-                        nc.vector.tensor_tensor(out=A[:, ds], in0=A[:, ds], in1=A[:, ss], op=ADD)
+                        ds, ss = slice(j - 3, 2 * j - 7), slice(j - 5, None, -1)
+                    nc.vector.tensor_tensor(out=A[:, ds], in0=A[:, ds], in1=A[:, ss], op=ADD)
+
+            def place(im):
+                dst = Pv[:, :, 0:7, 65 * im:65 * im + 64].rearrange("p x y (j i) -> p x y j i", i=8)
+                nc.scalar.copy(out=dst, in_=D[:, im, ::-1, ::-1].rearrange("p y x i j -> p x y j i"))
+
+            def pfold(im):
+                colfold(lambda j: Pv[:, :, 0:7, 65 * im + 8 * j:65 * im + 8 * j + 8])
+
+            def zprep(n):
+                expo(n, Dz[:])
+
+            def zfold():
+                rowfold(Dz, False)
+                v = Dz[:].rearrange("p y x i j -> p x y i j")
+                for j in (0, 1, 2, 5, 6, 7):
+                    A = v[:, :, :, :, j]
+                    if j < 3:
+                        ds, ss = slice(4 - j, 7 - 2 * j), slice(2 - j, None, -1)
+                    else:
+                        ds, ss = slice(14 - 2 * j, 10 - j), slice(6, 10 - j, -1)
+                    nc.vector.tensor_tensor(out=A[:, ds], in0=A[:, ds], in1=A[:, ss], op=ADD)
+
+            zacc = {}
+
+            def zstream(n):
+                zq, im = divmod(n - 12, 2)
+                if im == 0:
+                    zacc[zq] = pool.tile([128, 8, 2, 8, 8], F32, name="zacc", bufs=1)
+                acc = zacc[zq]
+                gz = gzs[n]
+                offs = [(dy, dx) for dy in range(7) for dx in range(7) if (dy, dx) != (3, 3)]
+                tmps = {}
+
+                def rect(d):
+                    return max(0, 3 - d), min(8, 11 - d)
+
+                def mul(k):
+                    dy, dx = offs[k]
+                    i0, i1 = rect(dy)
+                    j0, j1 = rect(dx)
+                    t = pool.tile([128, 8, 8, 8], F32, name="ztmp", bufs=2)
+                    nc.vector.tensor_tensor(
+                        out=t[:, :, 0:i1 - i0, 0:j1 - j0], in0=gz[:, :, i0:i1, j0:j1],
+                        in1=Dz[:, dy, dx:dx + 1, i0:i1, j0:j1].to_broadcast([128, 8, i1 - i0, j1 - j0]), op=MUL)
+                    tmps[k] = t
+
+                def add(k):
+                    dy, dx = offs[k]
+                    i0, i1 = rect(dy)
+                    j0, j1 = rect(dx)
+                    a = acc[:, :, im, i0 + dy - 3:i1 + dy - 3, j0 + dx - 3:j1 + dx - 3]
+                    nc.vector.tensor_tensor(out=a, in0=a, in1=tmps.pop(k)[:, :, 0:i1 - i0, 0:j1 - j0], op=ADD)
+
+                def first():
+                    nc.vector.tensor_tensor(
+                        out=acc[:, :, im], in0=gz[:],
+                        in1=Dz[:, 3, 3:4].to_broadcast([128, 8, 8, 8]), op=MUL)
+
+                todo = [first, lambda: mul(0)]
+                for k in range(48):
+                    if k + 1 < 48:
+                        todo.append(lambda k=k: mul(k + 1))
+                    todo.append(lambda k=k: add(k))
+                return todo
+
+            def zdone(zq):
+                acc = zacc[zq]
+                dzz = pool.tile([128, 4, 256], F32, name="dzz", bufs=1)
+                for t2 in range(2):
+                    zb = psA.tile([128, 2, 2, 128], F32, name="aux")
+                    for tt in range(2):
+                        for ch in range(2):
+                            nc.tensor.transpose(
+                                zb[:, tt, ch, :], acc[:, 4 * ch + 2 * t2 + tt].rearrange("p m i j -> p (m i j)"), identf[:])
+                    nc.scalar.copy(out=dzz[:, 2 * t2:2 * t2 + 2, :].rearrange("p t (h c) -> p t h c", c=2),
+                                   in_=zb[:].rearrange("p t c h -> p t h c"))
+                for g in range(2):
+                    zb = psA.tile([128, 4, 128], F32, name="aux")
+                    for t in range(4):
+                        nc.tensor.transpose(zb[:, t, :], dzz[:, t, 128 * g:128 * g + 128], identf[:])
+                    k0 = 128 * (XG + zq)
+                    nc.scalar.copy(out=qf[g][:, k0:k0 + 128, :], in_=zb[:].rearrange("p t n -> p n t"))
 
             gms = {}
 
@@ -114,27 +200,24 @@ def tile_sam_pb_v_kernel(tc, logits, x, w3c, b3c, lse, grad_out, out_0, out_1):
                 gl = gls[q]
                 gr = pool.tile([128, 4, 2, 8, 8, 2], BF16, name="gr", bufs=1)
                 for cl in range(4):
-                    nc.vector.tensor_copy(
+                    nc.scalar.copy(
                         out=gr[:, cl],
                         in_=gl[:].rearrange("p m (a b) i j -> p b a j i m", b=4)[:, cl])
                 gt = psA.tile([128, 8, 128], BF16, name="aux")
                 grv = gr[:].rearrange("p b a j i m -> p (b a) (j i m)")
                 for c in range(8):
                     nc.tensor.transpose(gt[:, c, :], grv[:, c, :], identb[:])
-                gx = pool.tile([128, 64, 2, 8], BF16, name="gx", bufs=2)
+                gx = pool.tile([128, 128, 2, 8], BF16, name="gx", bufs=1)
                 for im in range(2):
                     nc.scalar.activation(
-                        out=gx[:, :, im, :], in_=gt[:, :, 0:64].rearrange("p c r -> p r c"),
+                        out=gx[:, :, im, :], in_=gt[:].rearrange("p c r -> p r c"),
                         func=COPY, scale=par[:, im:im + 1])
-                gy = pool.tile([128, 64, 8], F32, name="gy", bufs=2)
-                nc.vector.tensor_copy(out=gy[:], in_=gt[:, :, 64:128].rearrange("p c r -> p r c"))
-                gms[q] = (gx, gy)
+                gms[q] = gx
 
             wms = {}
 
             def tstage(q, extra):
-                wx = pool.tile([128, 2, 64, 64], BF16, name="wx", bufs=1)
-                wy = pool.tile([128, 64, 128], F32, name="wy", bufs=1)
+                wx = pool.tile([128, 2, 64, 128], BF16, name="wx", bufs=1)
                 for k in range(16):
                     tb = psT.tile([128, 4, 128], F32, name="tb")
                     for a in range(4):
@@ -142,75 +225,57 @@ def tile_sam_pb_v_kernel(tc, logits, x, w3c, b3c, lse, grad_out, out_0, out_1):
                         s = BASE + PITCH * (27 - (8 * j + i))
                         nc.tensor.transpose(tb[:, a, :], P[:, s:s + 65 * 127 + 1:65], identf[:])
                     hi = wx[:, 0, 4 * k:4 * k + 4, :]
-                    lo = wx[:, 1, 4 * k:4 * k + 4, :]
-                    nc.scalar.copy(out=hi, in_=tb[:, :, 0:64])
-                    tv = tb[:, :, 64:128].rearrange("p a r -> p r a")
-                    nc.scalar.activation(out=wy[:, :, 4 * k:4 * k + 4], in_=tv, func=COPY, scale=par[:, 0:1])
-                    nc.vector.tensor_tensor(out=lo, in0=tb[:, :, 0:64], in1=hi, op=SUB)
-                    nc.vector.tensor_scalar(out=wy[:, :, 64 + 4 * k:64 + 4 * k + 4], in0=tv,
-                                            scalar1=par[:, 1:2], scalar2=None, op0=MUL)
-                    for f in extra.get(k, ()):
+                    nc.scalar.copy(out=hi, in_=tb[:])
+                    nc.vector.tensor_tensor(out=wx[:, 1, 4 * k:4 * k + 4, :], in0=tb[:], in1=hi, op=SUB)
+                    for f in extra(k):
                         f()
-                wms[q] = (wx, wy)
+                wms[q] = wx
 
             dzs = {}
 
-            def mstage(q):
-                gx, gy = gms[q]
-                wx, wy = wms[q]
-                wxv = wx[:].rearrange("p a n r -> p (a n) r")
-                dzx = pool.tile([128, 8, 128], F32, name="dzx", bufs=1)
-                for s in range(2):
+            def mstage(q, before, extra):
+                gx = gms[q]
+                wxv = wms[q][:].rearrange("p a n r -> p (a n) r")
+                dzx = pool.tile([128, 2, 8, 128], F32, name="dzx", bufs=1)
+                for s in range(4):
+                    before(s)
                     mb = psM.tile([128, 8, 64], F32, name="mb")
                     for r in range(32):
                         nc.tensor.matmul(
                             mb[:, :, 2 * r:2 * r + 2], lhsT=wxv[:, :, 32 * s + r],
                             rhs=gx[:, 32 * s + r].rearrange("p m c -> p (m c)"), start=True, stop=True)
-                    nc.scalar.copy(out=dzx[:, :, 64 * s:64 * s + 64], in_=mb[:])
-                    if q + 2 < 8:
-                        expo(q + 2, s)
-                dzy = pool.tile([128, 4, 128], F32, name="dzy", bufs=1)
-                mb = psM.tile([128, 4, 128], F32, name="mb")
-                for r in range(64):
-                    nc.tensor.matmul(mb[:, :, 2 * r:2 * r + 2], lhsT=wy[:, r, :], rhs=gy[:, r, :],
-                                     start=True, stop=True)
-                nc.scalar.copy(out=dzy[:], in_=mb[:])
-                dzs[q] = (dzx, dzy)
+                    nc.scalar.copy(out=dzx[:, s // 2, :, 64 * (s % 2):64 * (s % 2) + 64], in_=mb[:])
+                    for f in extra(s):
+                        f()
+                dzs[q] = dzx
 
-            def dz_split(q, im):
-                dzx, dzy = dzs[q]
+            def dz_split(q, g, im):
+                dzx = dzs[q]
                 zb = psA.tile([128, 4, 128], F32, name="aux")
                 for t in range(4):
-                    nc.tensor.transpose(zb[:, t, :], dzx[:, 4 * im + t, :], identf[:])
+                    nc.tensor.transpose(zb[:, t, :], dzx[:, g, 4 * im + t, :], identf[:])
                 k0 = 128 * q + 64 * im
                 with nc.allow_low_precision(reason="dz is rounded once to bfloat16"):
                     nc.vector.tensor_reduce(
-                        qf[0][:, k0:k0 + 64, :],
+                        qf[g][:, k0:k0 + 64, :],
                         zb[:].rearrange("p t (a n) -> p n t a", a=2), axis=AX, op=ADD)
 
-            def dz_whole(q):
-                dzx, dzy = dzs[q]
-                zb = psA.tile([128, 4, 128], F32, name="aux")
-                for t in range(4):
-                    nc.tensor.transpose(zb[:, t, :], dzy[:, t, :], identf[:])
-                nc.scalar.copy(out=qf[1][:, 128 * q:128 * q + 128, :], in_=zb[:].rearrange("p t n -> p n t"))
-
-            def wprep(q):
-                g, cq = divmod(q, 4)
-                wl = pool.tile([128, 4, 256], BF16, name="wl", bufs=1)
+            def wprep(n):
+                g, cq = divmod(n, 4)
+                wl = pool.tile([128, 4, 256], BF16, name="wl", bufs=2)
                 cols = slice(256 * cq, 256 * cq + 256)
                 nc.sync.dma_start(
                     out=wl[:], in_=w3c.rearrange("(g p j) w -> g p j w", g=2, j=4)[g][:, :, cols])
-                wi = pool.tile([128, 256, 4], BF16, name="wi", bufs=1, align_bytes=64)
-                nc.vector.tensor_copy(out=wi[:], in_=wl[:].rearrange("p j w -> p w j"))
+                wi = pool.tile([128, 256, 4], BF16, name="wi", bufs=2, align_bytes=64)
+                nc.scalar.copy(out=wi[:], in_=wl[:].rearrange("p j w -> p w j"))
                 nc.vector.quantize_mx(out=wc[g][:, cols].bitcast(E4X4), scales=ws[g][:, cols],
                                       in_=wi[:].rearrange("p w j -> p (w j)"))
 
-            def xprep(q):
+            def xprep(n):
                 xi = pool.tile([128, 2, 128, 4], BF16, name="xi", bufs=1, align_bytes=64)
-                xl = pool.tile([128, 16, 64], BF16, name="xl", bufs=2)
+                xl = pool.tile([128, 16, 64], BF16, name="xl", bufs=1)
                 nc.sync.dma_start(
-                    out=xl[:], in_=x.rearrange("b (k c) i j -> k c b (i j)", c=128)[q])
+                    out=xl[:], in_=x.rearrange("b (k c) i j -> k c b (i j)", c=128)[n])
                 xw = xl[:].rearrange("p b n -> p (b n)").bitcast(F32)
                 xb = psA.tile([128, 4, 128], F32, name="aux")
                 for hv in range(4):
@@ -220,40 +285,99 @@ def tile_sam_pb_v_kernel(tc, logits, x, w3c, b3c, lse, grad_out, out_0, out_1):
                     nc.scalar.copy(
                         out=xi[:, h].rearrange("p c u -> p (c u)").bitcast(F32).rearrange("p (c v) -> p c v", v=2),
                         in_=xb[:, 2 * h:2 * h + 2, :].rearrange("p v c -> p c v"))
-                    cols = slice(128 * q, 128 * q + 128)
+                    cols = slice(128 * n, 128 * n + 128)
                     nc.vector.quantize_mx(out=xc[h][:, cols].bitcast(E4X4), scales=xs[h][:, cols],
                                           in_=xi[:, h].rearrange("p c u -> p (c u)"))
 
-            for n in range(3):
-                load_logits(n)
+            load_logits()
+            nc.sync.dma_start(out=lset[:], in_=lse.rearrange("b h n -> h b n"))
+            load_logits()
+            load_logits()
             load_grad(0)
+            nc.gpsimd.memset(P[:, 0:BASE], 0.0)
+            nc.vector.memset(P[:, BASE + 55 * PITCH:PLEN], 0.0)
+            nc.vector.memset(Pv[:, :, 7, :], 0.0)
+            skip = None
             with tc.manual_schedule():
-                for im in range(2):
-                    expo(0, im)
-                    rowfold(0, im)
+                expo(0, D[:, 0])
+                expo(1, D[:, 1])
+                zprep(12)
+                rowfold(D[:, 0], True)
                 place(0)
-                for im in range(2):
-                    expo(1, im)
-                for q in range(8):
+                rowfold(D[:, 1], True)
+                place(1)
+                zfold()
+                todo = zstream(12)
+                for n in (13, 14, 15):
+                    if n == 14:
+                        todo.append(lambda: zdone(0))
+                    todo.append(lambda n=n: zprep(n))
+                    todo.extend([skip, skip, skip, zfold])
+                    todo.append(lambda n=n: insert(zstream(n)))
+
+                def insert(items):
+                    rest = todo[:]
+                    todo.clear()
+                    todo.extend(items + rest)
+
+                def zrun(n):
+                    for c in range(n):
+                        if not todo:
+                            return
+                        f = todo[0]
+                        rest = todo[1:]
+                        todo.clear()
+                        todo.extend(rest)
+                        if f is None:
+                            return
+                        f()
+
+                zrun(6)
+                pfold(0)
+                zrun(4)
+                pfold(1)
+                expo(2, D[:, 0])
+                expo(3, D[:, 1])
+                for q in range(XG):
                     load_grad(q + 1)
-                    extra = {k: [] for k in range(16)}
-                    extra[9].append(lambda: gprep(q))
-                    if q > 0:
-                        extra[1].append(lambda: dz_split(q - 1, 0))
-                        extra[3].append(lambda: dz_split(q - 1, 1))
-                        extra[5].append(lambda: dz_whole(q - 1))
-                    if q < 7:
-                        extra[4].append(lambda: rowfold(q + 1, 0))
-                        extra[7].append(lambda: rowfold(q + 1, 1))
-                    extra[11].append(lambda: wprep(q))
-                    extra[13].append(lambda: xprep(q))
-                    tstage(q, extra)
-                    if q < 7:
-                        place(q + 1)
-                    mstage(q)
-                for im in range(2):
-                    dz_split(7, im)
-                dz_whole(7)
+
+                    def during_t(k):
+                        out = [lambda: zrun(NZT)]
+                        if k in (2, 4, 6, 8) and q > 0:
+                            g, im = divmod(k // 2 - 1, 2)
+                            out.append(lambda: dz_split(q - 1, g, im))
+                        if k in (5, 9) and q + 1 < XG:
+                            out.append(lambda: rowfold(D[:, (k - 5) // 4], True))
+                        if k == 10:
+                            out.append(lambda: gprep(q))
+                        if k in (12, 13) and q < 4:
+                            out.append(lambda: wprep(2 * q + k - 12))
+                        if k in (14, 15) and 0 < q < 5:
+                            out.append(lambda: xprep(2 * q - 2 + k - 14))
+                        return out
+
+                    tstage(q, during_t)
+
+                    def before_m(s):
+                        if s < 2 and q + 1 < XG:
+                            place(s)
+                        if s > 1 and q + 2 < XG:
+                            expo(2 * q + 2 + s, D[:, s - 2])
+
+                    def during_m(s):
+                        if s < 2 and q + 1 < XG:
+                            return [lambda: zrun(NZM), lambda: pfold(s)]
+                        return [lambda: zrun(NZM)]
+
+                    mstage(q, before_m, during_m)
+                zrun(1000)
+                zrun(1000)
+                zrun(1000)
+                zrun(1000)
+                for g in range(2):
+                    for im in range(2):
+                        dz_split(XG - 1, g, im)
+                zdone(1)
 
         with ExitStack() as ectx:
             fin = ectx.enter_context(tc.tile_pool(name="fin", bufs=2))

@@ -23,7 +23,7 @@ BASE = 36 * PITCH
 PLEN = 16384
 XG = 6
 NZT = 3
-NZM = 5
+NZM = 8
 
 
 def tile_sam_pb_v_kernel(tc, logits, x, w3c, b3c, lse, grad_out, out_0, out_1):
@@ -32,6 +32,9 @@ def tile_sam_pb_v_kernel(tc, logits, x, w3c, b3c, lse, grad_out, out_0, out_1):
         keep = ctx.enter_context(tc.tile_pool(name="keep", bufs=1))
         identf = keep.tile([128, 128], F32, name="identf")
         make_identity(nc, identf[:])
+        swapf = keep.tile([128, 128], F32, name="swapf")
+        nc.vector.tensor_copy(out=swapf[:, 0:64], in_=identf[:, 64:128])
+        nc.vector.tensor_copy(out=swapf[:, 64:128], in_=identf[:, 0:64])
         identb = keep.tile([128, 128], BF16, name="identb")
         make_identity(nc, identb[:])
         par = keep.tile([128, 2], F32, name="par")
@@ -42,6 +45,58 @@ def tile_sam_pb_v_kernel(tc, logits, x, w3c, b3c, lse, grad_out, out_0, out_1):
         ws = [keep.tile([128, 1024], U8, name="ws%d" % g, align_bytes=64) for g in range(2)]
         xc = [keep.tile([128, 1024], U32, name="xc%d" % g, align_bytes=64) for g in range(2)]
         xs = [keep.tile([128, 1024], U8, name="xs%d" % g, align_bytes=64) for g in range(2)]
+
+        qc = [[keep.tile([128, 512], U32, name="qc%d" % g, align_bytes=64)] for g in range(2)]
+        qs = [[keep.tile([128, 512], U8, name="qs%d" % g, align_bytes=64)] for g in range(2)]
+        tcod = [keep.tile([128, 1024], U32, name="tc0", align_bytes=64)]
+        tsc = [keep.tile([128, 1024], U8, name="ts0", align_bytes=64)]
+        o0 = out_0.rearrange("b (k c) i j -> k c b (i j)", c=128)
+        o1 = out_1.rearrange("(g p t) w -> g t p w", g=2, t=4)
+
+        def code_features(h):
+            for g in range(2):
+                nc.vector.quantize_mx(
+                    out=qc[g][h][:].bitcast(E5X4), scales=qs[g][h][:],
+                    in_=qf[g][:, 512 * h:512 * h + 512, :].rearrange("p k t -> p (k t)"))
+
+        qts = {}
+
+        def turn_tokens(h, g, t, ps, tag, store, eng):
+            if t == 0:
+                qts[(h, g)] = store.tile([128, 4, 128, 4], BF16, name="qt", align_bytes=64, bufs=1 if h == 0 else 2)
+            qt = qts[(h, g)]
+            tb = ps.tile([128, 4, 128], BF16, name=tag)
+            for u in range(4):
+                nc.tensor.transpose(tb[:, u, :], qf[g][:, 512 * h + u:512 * h + 512:4, t], identb[:])
+            eng(out=qt[:, t], in_=tb[:].rearrange("p u o -> p o u"))
+
+        def code_tokens(h, g):
+            cols = slice(512 * g, 512 * g + 512)
+            nc.vector.quantize_mx(out=tcod[h][:, cols].bitcast(E5X4), scales=tsc[h][:, cols],
+                                  in_=qts[(h, g)][:].rearrange("p t o u -> p (t o u)"))
+
+        def gradient_x(h, k, ps, tag, store, stag, sbufs, eng):
+            acc = ps.tile([128, 512], F32, name=tag)
+            for g in range(2):
+                nc.tensor.matmul_mx(
+                    out=acc[:], lhsT=wc[g][:, 128 * k:128 * k + 128].bitcast(E4X4),
+                    lhsT_scale=ws[g][:, 128 * k:128 * k + 128],
+                    rhs=qc[g][h][:].bitcast(E5X4), rhs_scale=qs[g][h][:], start=(g == 0), stop=(g == 1))
+            st = store.tile([128, 512], F32, name=stag, bufs=sbufs)
+            eng(out=st[:], in_=acc[:])
+            nc.sync.dma_start(out=o0[k][:, 8 * h:8 * h + 8, :], in_=st[:].rearrange("p (b n) -> p b n", n=64))
+
+        def gradient_w(gt, ch, ps, tag, store, stag, sbufs, eng):
+            acc = ps.tile([128, 512], F32, name=tag)
+            for h in range(2):
+                nc.tensor.matmul_mx(
+                    out=acc[:], lhsT=tcod[h][:, 128 * gt:128 * gt + 128].bitcast(E5X4),
+                    lhsT_scale=tsc[h][:, 128 * gt:128 * gt + 128],
+                    rhs=xc[h][:, 512 * ch:512 * ch + 512].bitcast(E4X4),
+                    rhs_scale=xs[h][:, 512 * ch:512 * ch + 512], start=(h == 0), stop=(h == 1))
+            st = store.tile([128, 512], F32, name=stag, bufs=sbufs)
+            eng(out=st[:], in_=acc[:])
+            nc.sync.dma_start(out=o1[gt // 4][gt % 4][:, 512 * ch:512 * ch + 512], in_=st[:])
 
         with ExitStack() as mctx:
             big = mctx.enter_context(tc.tile_pool(name="big", bufs=1))
@@ -59,38 +114,39 @@ def tile_sam_pb_v_kernel(tc, logits, x, w3c, b3c, lse, grad_out, out_0, out_1):
             lgs = {}
             gls = {}
             gzs = {}
-            order = [0, 1, 12, 2, 3, 4, 5, 13, 6, 7, 8, 9, 14, 10, 11, 15]
+            order = [0, 1, 12, 2, 3, 4, 5, 13, 6, 7, 14, 8, 9, 10, 11, 15]
             loaded = [0]
 
             def load_logits():
                 if loaded[0] < 16:
                     n = order[loaded[0]]
                     loaded[0] += 1
-                    t = pool.tile([128, 49, 64], BF16, name="lg", bufs=3)
+                    t = pool.tile([128, 49, 64], BF16, name="lg", bufs=2)
                     nc.sync.dma_start(out=t[:], in_=logits[n])
                     lgs[n] = t
                     if n >= 12:
-                        t = pool.tile([128, 8, 8, 8], BF16, name="gz", bufs=2)
-                        nc.sync.dma_start(out=t[:].rearrange("p c i j -> p (c i j)"),
+                        t = pool.tile([128, 8, 64], BF16, name="gz", bufs=1)
+                        nc.sync.dma_start(out=t[:].rearrange("p c n -> p (c n)"),
                                           in_=grad_out[n].rearrange("(h c) i j -> h (c i j)", c=8))
                         gzs[n] = t
 
             def load_grad(q):
                 if q < XG:
-                    t = pool.tile([128, 2, 8, 8, 8], BF16, name="gl", bufs=2)
+                    t = pool.tile([128, 2, 8, 8, 8], BF16, name="gl", bufs=1)
                     for im in range(2):
                         nc.sync.dma_start(
                             out=t[:, im].rearrange("p c i j -> p (c i j)"),
                             in_=grad_out[2 * q + im].rearrange("(h c) i j -> h (c i j)", c=8))
                     gls[q] = t
 
-            def expo(n, dst):
-                dv = dst.rearrange("p y x i j -> p (y x) (i j)")
+            def expo(n, dst, y0=0, y1=7):
+                dv = dst[:, y0:y1].rearrange("p y x i j -> p (y x) (i j)")
                 nc.vector.tensor_tensor(
-                    out=dv, in0=lgs[n][:],
-                    in1=lset[:, n:n + 1, :].to_broadcast([128, 49, 64]), op=SUB)
+                    out=dv, in0=lgs[n][:, 7 * y0:7 * y1, :],
+                    in1=lset[:, n:n + 1, :].to_broadcast([128, 7 * (y1 - y0), 64]), op=SUB)
                 nc.scalar.activation(out=dv, in_=dv, func=EXP)
-                load_logits()
+                if y1 == 7:
+                    load_logits()
 
             def rowfold(dst, clear):
                 for i in (0, 1, 2, 5, 6, 7):
@@ -99,7 +155,7 @@ def tile_sam_pb_v_kernel(tc, logits, x, w3c, b3c, lse, grad_out, out_0, out_1):
                         ds, ss, dead = slice(4 - i, 7 - 2 * i), slice(2 - i, None, -1), slice(0, 3 - i)
                     else:
                         ds, ss, dead = slice(14 - 2 * i, 10 - i), slice(6, 10 - i, -1), slice(11 - i, 7)
-                    nc.vector.tensor_tensor(out=A[:, ds], in0=A[:, ds], in1=A[:, ss], op=ADD)
+                    nc.gpsimd.tensor_tensor(out=A[:, ds], in0=A[:, ds], in1=A[:, ss], op=ADD)
                     if clear:
                         nc.gpsimd.memset(A[:, dead], 0.0)
 
@@ -112,15 +168,18 @@ def tile_sam_pb_v_kernel(tc, logits, x, w3c, b3c, lse, grad_out, out_0, out_1):
                         ds, ss = slice(j - 3, 2 * j - 7), slice(j - 5, None, -1)
                     nc.vector.tensor_tensor(out=A[:, ds], in0=A[:, ds], in1=A[:, ss], op=ADD)
 
-            def place(im):
+            def place(im, eng=nc.scalar.copy):
                 dst = Pv[:, :, 0:7, 65 * im:65 * im + 64].rearrange("p x y (j i) -> p x y j i", i=8)
-                nc.scalar.copy(out=dst, in_=D[:, im, ::-1, ::-1].rearrange("p y x i j -> p x y j i"))
+                eng(out=dst, in_=D[:, im, ::-1, ::-1].rearrange("p y x i j -> p x y j i"))
 
             def pfold(im):
                 colfold(lambda j: Pv[:, :, 0:7, 65 * im + 8 * j:65 * im + 8 * j + 8])
 
             def zprep(n):
                 expo(n, Dz[:])
+                t = pool.tile([128, 8, 8, 8], BF16, name="gzt", bufs=1)
+                nc.scalar.copy(out=t[:].rearrange("p i j c -> p (i j) c"), in_=gzs[n][:].rearrange("p c n -> p n c"))
+                gzs[n] = t
 
             def zfold():
                 rowfold(Dz, False)
@@ -131,14 +190,14 @@ def tile_sam_pb_v_kernel(tc, logits, x, w3c, b3c, lse, grad_out, out_0, out_1):
                         ds, ss = slice(4 - j, 7 - 2 * j), slice(2 - j, None, -1)
                     else:
                         ds, ss = slice(14 - 2 * j, 10 - j), slice(6, 10 - j, -1)
-                    nc.vector.tensor_tensor(out=A[:, ds], in0=A[:, ds], in1=A[:, ss], op=ADD)
+                    nc.gpsimd.tensor_tensor(out=A[:, ds], in0=A[:, ds], in1=A[:, ss], op=ADD)
 
             zacc = {}
 
             def zstream(n):
                 zq, im = divmod(n - 12, 2)
                 if im == 0:
-                    zacc[zq] = pool.tile([128, 8, 2, 8, 8], F32, name="zacc", bufs=1)
+                    zacc[zq] = pool.tile([128, 2, 8, 8, 8], F32, name="zacc", bufs=1)
                 acc = zacc[zq]
                 gz = gzs[n]
                 offs = [(dy, dx) for dy in range(7) for dx in range(7) if (dy, dx) != (3, 3)]
@@ -153,21 +212,21 @@ def tile_sam_pb_v_kernel(tc, logits, x, w3c, b3c, lse, grad_out, out_0, out_1):
                     j0, j1 = rect(dx)
                     t = pool.tile([128, 8, 8, 8], F32, name="ztmp", bufs=2)
                     nc.vector.tensor_tensor(
-                        out=t[:, :, 0:i1 - i0, 0:j1 - j0], in0=gz[:, :, i0:i1, j0:j1],
-                        in1=Dz[:, dy, dx:dx + 1, i0:i1, j0:j1].to_broadcast([128, 8, i1 - i0, j1 - j0]), op=MUL)
+                        out=t[:, 0:i1 - i0, 0:j1 - j0], in0=gz[:, i0:i1, j0:j1],
+                        in1=Dz[:, dy, dx, i0:i1, j0:j1].unsqueeze(3).to_broadcast([128, i1 - i0, j1 - j0, 8]), op=MUL)
                     tmps[k] = t
 
                 def add(k):
                     dy, dx = offs[k]
                     i0, i1 = rect(dy)
                     j0, j1 = rect(dx)
-                    a = acc[:, :, im, i0 + dy - 3:i1 + dy - 3, j0 + dx - 3:j1 + dx - 3]
-                    nc.vector.tensor_tensor(out=a, in0=a, in1=tmps.pop(k)[:, :, 0:i1 - i0, 0:j1 - j0], op=ADD)
+                    a = acc[:, im, i0 + dy - 3:i1 + dy - 3, j0 + dx - 3:j1 + dx - 3]
+                    nc.vector.tensor_tensor(out=a, in0=a, in1=tmps.pop(k)[:, 0:i1 - i0, 0:j1 - j0], op=ADD)
 
                 def first():
                     nc.vector.tensor_tensor(
-                        out=acc[:, :, im], in0=gz[:],
-                        in1=Dz[:, 3, 3:4].to_broadcast([128, 8, 8, 8]), op=MUL)
+                        out=acc[:, im], in0=gz[:],
+                        in1=Dz[:, 3, 3].unsqueeze(3).to_broadcast([128, 8, 8, 8]), op=MUL)
 
                 todo = [first, lambda: mul(0)]
                 for k in range(48):
@@ -178,13 +237,14 @@ def tile_sam_pb_v_kernel(tc, logits, x, w3c, b3c, lse, grad_out, out_0, out_1):
 
             def zdone(zq):
                 acc = zacc[zq]
-                dzz = pool.tile([128, 4, 256], F32, name="dzz", bufs=1)
+                dzz = pool.tile([128, 4, 256], F32, name="qt", align_bytes=64, bufs=1)
                 for t2 in range(2):
                     zb = psA.tile([128, 2, 2, 128], F32, name="aux")
                     for tt in range(2):
                         for ch in range(2):
                             nc.tensor.transpose(
-                                zb[:, tt, ch, :], acc[:, 4 * ch + 2 * t2 + tt].rearrange("p m i j -> p (m i j)"), identf[:])
+                                zb[:, tt, ch, :],
+                                acc[:].rearrange("p m i j c -> p c (m i j)")[:, 4 * ch + 2 * t2 + tt, :], identf[:])
                     nc.scalar.copy(out=dzz[:, 2 * t2:2 * t2 + 2, :].rearrange("p t (h c) -> p t h c", c=2),
                                    in_=zb[:].rearrange("p t c h -> p t h c"))
                 for g in range(2):
@@ -226,9 +286,9 @@ def tile_sam_pb_v_kernel(tc, logits, x, w3c, b3c, lse, grad_out, out_0, out_1):
                         nc.tensor.transpose(tb[:, a, :], P[:, s:s + 65 * 127 + 1:65], identf[:])
                     hi = wx[:, 0, 4 * k:4 * k + 4, :]
                     nc.scalar.copy(out=hi, in_=tb[:])
-                    nc.vector.tensor_tensor(out=wx[:, 1, 4 * k:4 * k + 4, :], in0=tb[:], in1=hi, op=SUB)
                     for f in extra(k):
                         f()
+                    nc.vector.tensor_tensor(out=wx[:, 1, 4 * k:4 * k + 4, :], in0=tb[:], in1=hi, op=SUB)
                 wms[q] = wx
 
             dzs = {}
@@ -253,27 +313,33 @@ def tile_sam_pb_v_kernel(tc, logits, x, w3c, b3c, lse, grad_out, out_0, out_1):
                 dzx = dzs[q]
                 zb = psA.tile([128, 4, 128], F32, name="aux")
                 for t in range(4):
-                    nc.tensor.transpose(zb[:, t, :], dzx[:, g, 4 * im + t, :], identf[:])
+                    nc.tensor.matmul(zb[:, t, :], lhsT=dzx[:, g, 4 * im + t, :], rhs=identf[:],
+                                     start=True, stop=False, is_transpose=True)
+                    nc.tensor.matmul(zb[:, t, :], lhsT=dzx[:, g, 4 * im + t, :], rhs=swapf[:],
+                                     start=False, stop=True, is_transpose=True)
+                zbs[(q, g, im)] = zb
+
+            zbs = {}
+
+            def dz_round(q, g, im):
+                zb = zbs[(q, g, im)]
                 k0 = 128 * q + 64 * im
-                with nc.allow_low_precision(reason="dz is rounded once to bfloat16"):
-                    nc.vector.tensor_reduce(
-                        qf[g][:, k0:k0 + 64, :],
-                        zb[:].rearrange("p t (a n) -> p n t a", a=2), axis=AX, op=ADD)
+                nc.scalar.copy(out=qf[g][:, k0:k0 + 64, :], in_=zb[:, :, 0:64].rearrange("p t n -> p n t"))
 
             def wprep(n):
                 g, cq = divmod(n, 4)
-                wl = pool.tile([128, 4, 256], BF16, name="wl", bufs=2)
+                wl = pool.tile([128, 4, 256], BF16, name="io", bufs=2)
                 cols = slice(256 * cq, 256 * cq + 256)
                 nc.sync.dma_start(
                     out=wl[:], in_=w3c.rearrange("(g p j) w -> g p j w", g=2, j=4)[g][:, :, cols])
-                wi = pool.tile([128, 256, 4], BF16, name="wi", bufs=2, align_bytes=64)
+                wi = pool.tile([128, 256, 4], BF16, name="iq", bufs=2, align_bytes=64)
                 nc.scalar.copy(out=wi[:], in_=wl[:].rearrange("p j w -> p w j"))
                 nc.vector.quantize_mx(out=wc[g][:, cols].bitcast(E4X4), scales=ws[g][:, cols],
                                       in_=wi[:].rearrange("p w j -> p (w j)"))
 
             def xprep(n):
-                xi = pool.tile([128, 2, 128, 4], BF16, name="xi", bufs=1, align_bytes=64)
-                xl = pool.tile([128, 16, 64], BF16, name="xl", bufs=1)
+                xi = pool.tile([128, 2, 128, 4], BF16, name="iq", bufs=2, align_bytes=64)
+                xl = pool.tile([128, 16, 64], BF16, name="io", bufs=2)
                 nc.sync.dma_start(
                     out=xl[:], in_=x.rearrange("b (k c) i j -> k c b (i j)", c=128)[n])
                 xw = xl[:].rearrange("p b n -> p (b n)").bitcast(F32)
@@ -292,27 +358,26 @@ def tile_sam_pb_v_kernel(tc, logits, x, w3c, b3c, lse, grad_out, out_0, out_1):
             load_logits()
             nc.sync.dma_start(out=lset[:], in_=lse.rearrange("b h n -> h b n"))
             load_logits()
-            load_logits()
             load_grad(0)
             nc.gpsimd.memset(P[:, 0:BASE], 0.0)
             nc.vector.memset(P[:, BASE + 55 * PITCH:PLEN], 0.0)
             nc.vector.memset(Pv[:, :, 7, :], 0.0)
             skip = None
             with tc.manual_schedule():
-                expo(0, D[:, 0])
-                expo(1, D[:, 1])
-                zprep(12)
-                rowfold(D[:, 0], True)
+                for im in range(2):
+                    for y in range(7):
+                        expo(im, D[:, im], y, y + 1)
+                    rowfold(D[:, im], True)
                 place(0)
-                rowfold(D[:, 1], True)
-                place(1)
+                place(1, nc.vector.tensor_copy)
+                zprep(12)
                 zfold()
                 todo = zstream(12)
                 for n in (13, 14, 15):
                     if n == 14:
                         todo.append(lambda: zdone(0))
                     todo.append(lambda n=n: zprep(n))
-                    todo.extend([skip, skip, skip, zfold])
+                    todo.extend([skip, skip, skip, zfold, skip, skip, skip, skip, skip])
                     todo.append(lambda n=n: insert(zstream(n)))
 
                 def insert(items):
@@ -332,9 +397,7 @@ def tile_sam_pb_v_kernel(tc, logits, x, w3c, b3c, lse, grad_out, out_0, out_1):
                             return
                         f()
 
-                zrun(6)
                 pfold(0)
-                zrun(4)
                 pfold(1)
                 expo(2, D[:, 0])
                 expo(3, D[:, 1])
@@ -343,13 +406,23 @@ def tile_sam_pb_v_kernel(tc, logits, x, w3c, b3c, lse, grad_out, out_0, out_1):
 
                     def during_t(k):
                         out = [lambda: zrun(NZT)]
-                        if k in (2, 4, 6, 8) and q > 0:
-                            g, im = divmod(k // 2 - 1, 2)
-                            out.append(lambda: dz_split(q - 1, g, im))
+                        if 0 < k < 10 and q > 0:
+                            g, im = divmod((k - 1) // 2, 2)
+                            if k % 2 == 1 and k < 9:
+                                out.append(lambda: dz_split(q - 1, g, im))
+                            if k % 2 == 0:
+                                out.append(lambda: dz_round(q - 1, g, im))
                         if k in (5, 9) and q + 1 < XG:
                             out.append(lambda: rowfold(D[:, (k - 5) // 4], True))
                         if k == 10:
                             out.append(lambda: gprep(q))
+                        if q == 5:
+                            if k == 10:
+                                out.append(lambda: code_features(0))
+                            if k % 5 < 4 and k < 10:
+                                out.append(lambda: turn_tokens(0, k // 5, k % 5, psA, "aux", pool, nc.scalar.copy))
+                            if k in (4, 9):
+                                out.append(lambda: code_tokens(0, k // 5))
                         if k in (12, 13) and q < 4:
                             out.append(lambda: wprep(2 * q + k - 12))
                         if k in (14, 15) and 0 < q < 5:
@@ -365,78 +438,40 @@ def tile_sam_pb_v_kernel(tc, logits, x, w3c, b3c, lse, grad_out, out_0, out_1):
                             expo(2 * q + 2 + s, D[:, s - 2])
 
                     def during_m(s):
-                        if s < 2 and q + 1 < XG:
-                            return [lambda: zrun(NZM), lambda: pfold(s)]
-                        return [lambda: zrun(NZM)]
+                        if 0 < s < 3 and q + 1 < XG:
+                            return [lambda: zrun(NZM), lambda: pfold(s - 1)]
+                        out = [lambda: zrun(NZM)]
+                        if q == 5:
+                            for k in (2 * s, 2 * s + 1):
+                                out.append(lambda k=k: gradient_x(0, k, psA, "aux", pool, "io", 2, nc.scalar.copy))
+                        return out
 
                     mstage(q, before_m, during_m)
-                zrun(1000)
-                zrun(1000)
-                zrun(1000)
-                zrun(1000)
+                while todo:
+                    zrun(1000)
                 for g in range(2):
                     for im in range(2):
                         dz_split(XG - 1, g, im)
+                        dz_round(XG - 1, g, im)
                 zdone(1)
 
         with ExitStack() as ectx:
             fin = ectx.enter_context(tc.tile_pool(name="fin", bufs=2))
             ps = ectx.enter_context(tc.psum_pool(name="ps", bufs=4))
-            qc = [[fin.tile([128, 512], U32, name="qc%d%d" % (g, h), align_bytes=64, bufs=1) for h in range(2)] for g in range(2)]
-            qs = [[fin.tile([128, 512], U8, name="qs%d%d" % (g, h), align_bytes=64, bufs=1) for h in range(2)] for g in range(2)]
-            tcod = [fin.tile([128, 1024], U32, name="tc%d" % h, align_bytes=64, bufs=1) for h in range(2)]
-            tsc = [fin.tile([128, 1024], U8, name="ts%d" % h, align_bytes=64, bufs=1) for h in range(2)]
-            turn = 0
-            for h in range(2):
+            for g in range(2):
+                qc[g].append(fin.tile([128, 512], U32, name="qcb%d" % g, align_bytes=64, bufs=1))
+                qs[g].append(fin.tile([128, 512], U8, name="qsb%d" % g, align_bytes=64, bufs=1))
+            tcod.append(fin.tile([128, 1024], U32, name="tc1", align_bytes=64, bufs=1))
+            tsc.append(fin.tile([128, 1024], U8, name="ts1", align_bytes=64, bufs=1))
+            engines = [nc.vector.tensor_copy, nc.scalar.copy]
+            with tc.manual_schedule():
+                code_features(1)
                 for g in range(2):
-                    nc.vector.quantize_mx(
-                        out=qc[g][h][:].bitcast(E5X4), scales=qs[g][h][:],
-                        in_=qf[g][:, 512 * h:512 * h + 512, :].rearrange("p k t -> p (k t)"))
-                    qt = fin.tile([128, 4, 128, 4], BF16, name="qt", align_bytes=64)
                     for t in range(4):
-                        tb = ps.tile([128, 4, 128], BF16, name="tt")
-                        for u in range(4):
-                            nc.tensor.transpose(tb[:, u, :], qf[g][:, 512 * h + u:512 * h + 512:4, t], identb[:])
-                        if t % 2 == 0:
-                            nc.vector.tensor_copy(out=qt[:, t], in_=tb[:].rearrange("p u o -> p o u"))
-                        else:
-                            nc.scalar.copy(out=qt[:, t], in_=tb[:].rearrange("p u o -> p o u"))
-                    cols = slice(512 * g, 512 * g + 512)
-                    nc.vector.quantize_mx(out=tcod[h][:, cols].bitcast(E5X4), scales=tsc[h][:, cols],
-                                          in_=qt[:].rearrange("p t o u -> p (t o u)"))
-
-            o0 = out_0.rearrange("b (k c) i j -> k c b (i j)", c=128)
-            o1 = out_1.rearrange("(g p t) w -> g t p w", g=2, t=4)
-
-            def emit(acc, dst, shape_b):
-                st = fin.tile([128, 512], F32, name="st", bufs=6)
-                if emitted[0] % 2 == 0:
-                    nc.vector.tensor_copy(out=st[:], in_=acc[:])
-                else:
-                    nc.scalar.copy(out=st[:], in_=acc[:])
-                emitted[0] += 1
-                if shape_b:
-                    nc.sync.dma_start(out=dst, in_=st[:].rearrange("p (b n) -> p b n", n=64))
-                else:
-                    nc.sync.dma_start(out=dst, in_=st[:])
-
-            emitted = [0]
-            for h in range(2):
-                for k in range(8):
-                    acc = ps.tile([128, 512], F32, name="acc")
-                    for g in range(2):
-                        nc.tensor.matmul_mx(
-                            out=acc[:], lhsT=wc[g][:, 128 * k:128 * k + 128].bitcast(E4X4),
-                            lhsT_scale=ws[g][:, 128 * k:128 * k + 128],
-                            rhs=qc[g][h][:].bitcast(E5X4), rhs_scale=qs[g][h][:], start=(g == 0), stop=(g == 1))
-                    emit(acc, o0[k][:, 8 * h:8 * h + 8, :], True)
-            for gt in range(8):
-                for ch in range(2):
-                    acc = ps.tile([128, 512], F32, name="acc")
-                    for h in range(2):
-                        nc.tensor.matmul_mx(
-                            out=acc[:], lhsT=tcod[h][:, 128 * gt:128 * gt + 128].bitcast(E5X4),
-                            lhsT_scale=tsc[h][:, 128 * gt:128 * gt + 128],
-                            rhs=xc[h][:, 512 * ch:512 * ch + 512].bitcast(E4X4),
-                            rhs_scale=xs[h][:, 512 * ch:512 * ch + 512], start=(h == 0), stop=(h == 1))
-                    emit(acc, o1[gt // 4][gt % 4][:, 512 * ch:512 * ch + 512], False)
+                        turn_tokens(1, g, t, ps, "tt", fin, engines[t % 2])
+                    for k in range(4 * g, 4 * g + 4):
+                        gradient_x(1, k, ps, "acc", fin, "st", 8, engines[k % 2])
+                    code_tokens(1, g)
+                for gt in range(8):
+                    for ch in range(2):
+                        gradient_w(gt, ch, ps, "acc", fin, "st", 8, engines[ch])

@@ -22,8 +22,8 @@ PITCH = 129
 BASE = 36 * PITCH
 PLEN = 16384
 XG = 6
-NZT = 3
-NZM = 8
+NZT = 2
+NZM = 5
 
 
 def tile_sam_pb_v_kernel(tc, logits, x, w3c, b3c, lse, grad_out, out_0, out_1):
@@ -114,7 +114,7 @@ def tile_sam_pb_v_kernel(tc, logits, x, w3c, b3c, lse, grad_out, out_0, out_1):
             lgs = {}
             gls = {}
             gzs = {}
-            order = [0, 1, 12, 2, 3, 4, 5, 13, 6, 7, 14, 8, 9, 10, 11, 15]
+            order = [0, 1, 12, 2, 3, 4, 5, 6, 13, 7, 8, 9, 14, 10, 11, 15]
             loaded = [0]
 
             def load_logits():
@@ -159,7 +159,7 @@ def tile_sam_pb_v_kernel(tc, logits, x, w3c, b3c, lse, grad_out, out_0, out_1):
                     if clear:
                         nc.gpsimd.memset(A[:, dead], 0.0)
 
-            def colfold(rows):
+            def colfold(rows, fill):
                 for j in (0, 1, 2, 5, 6, 7):
                     A = rows(j)
                     if j < 3:
@@ -167,13 +167,16 @@ def tile_sam_pb_v_kernel(tc, logits, x, w3c, b3c, lse, grad_out, out_0, out_1):
                     else:
                         ds, ss = slice(j - 3, 2 * j - 7), slice(j - 5, None, -1)
                     nc.vector.tensor_tensor(out=A[:, ds], in0=A[:, ds], in1=A[:, ss], op=ADD)
+                    fill(1)
 
             def place(im, eng=nc.scalar.copy):
-                dst = Pv[:, :, 0:7, 65 * im:65 * im + 64].rearrange("p x y (j i) -> p x y j i", i=8)
-                eng(out=dst, in_=D[:, im, ::-1, ::-1].rearrange("p y x i j -> p x y j i"))
+                for dx in range(7):
+                    dst = Pv[:, 6 - dx, 0:7, 65 * im:65 * im + 64].rearrange("p y (j i) -> p y i j", i=8)
+                    src = D[:, im, ::-1, dx]
+                    eng(out=dst.rearrange("p y i (a b) -> p y a i b", b=4), in_=src.rearrange("p y i (a b) -> p y a i b", b=4))
 
-            def pfold(im):
-                colfold(lambda j: Pv[:, :, 0:7, 65 * im + 8 * j:65 * im + 8 * j + 8])
+            def pfold(im, fill):
+                colfold(lambda j: Pv[:, :, 0:7, 65 * im + 8 * j:65 * im + 8 * j + 8], fill)
 
             def zprep(n):
                 expo(n, Dz[:])
@@ -210,7 +213,7 @@ def tile_sam_pb_v_kernel(tc, logits, x, w3c, b3c, lse, grad_out, out_0, out_1):
                     dy, dx = offs[k]
                     i0, i1 = rect(dy)
                     j0, j1 = rect(dx)
-                    t = pool.tile([128, 8, 8, 8], F32, name="ztmp", bufs=2)
+                    t = pool.tile([128, 8, 8, 8], F32, name="ztmp", bufs=4)
                     nc.vector.tensor_tensor(
                         out=t[:, 0:i1 - i0, 0:j1 - j0], in0=gz[:, i0:i1, j0:j1],
                         in1=Dz[:, dy, dx, i0:i1, j0:j1].unsqueeze(3).to_broadcast([128, i1 - i0, j1 - j0, 8]), op=MUL)
@@ -228,10 +231,10 @@ def tile_sam_pb_v_kernel(tc, logits, x, w3c, b3c, lse, grad_out, out_0, out_1):
                         out=acc[:, im], in0=gz[:],
                         in1=Dz[:, 3, 3].unsqueeze(3).to_broadcast([128, 8, 8, 8]), op=MUL)
 
-                todo = [first, lambda: mul(0)]
+                todo = [first, lambda: mul(0), lambda: mul(1)]
                 for k in range(48):
-                    if k + 1 < 48:
-                        todo.append(lambda k=k: mul(k + 1))
+                    if k + 2 < 48:
+                        todo.append(lambda k=k: mul(k + 2))
                     todo.append(lambda k=k: add(k))
                 return todo
 
@@ -363,7 +366,8 @@ def tile_sam_pb_v_kernel(tc, logits, x, w3c, b3c, lse, grad_out, out_0, out_1):
             nc.vector.memset(P[:, BASE + 55 * PITCH:PLEN], 0.0)
             nc.vector.memset(Pv[:, :, 7, :], 0.0)
             skip = None
-            with tc.manual_schedule():
+            kept = {mybir.EngineType.PE, mybir.EngineType.Pool, mybir.EngineType.SP}
+            with tc.manual_schedule(engines=kept):
                 for im in range(2):
                     for y in range(7):
                         expo(im, D[:, im], y, y + 1)
@@ -372,40 +376,29 @@ def tile_sam_pb_v_kernel(tc, logits, x, w3c, b3c, lse, grad_out, out_0, out_1):
                 place(1, nc.vector.tensor_copy)
                 zprep(12)
                 zfold()
-                todo = zstream(12)
-                for n in (13, 14, 15):
-                    if n == 14:
-                        todo.append(lambda: zdone(0))
-                    todo.append(lambda n=n: zprep(n))
-                    todo.extend([skip, skip, skip, zfold, skip, skip, skip, skip, skip])
-                    todo.append(lambda n=n: insert(zstream(n)))
-
-                def insert(items):
-                    rest = todo[:]
-                    todo.clear()
-                    todo.extend(items + rest)
-
                 def zrun(n):
-                    for c in range(n):
-                        if not todo:
-                            return
-                        f = todo[0]
-                        rest = todo[1:]
-                        todo.clear()
-                        todo.extend(rest)
-                        if f is None:
-                            return
-                        f()
+                    return n
 
-                pfold(0)
-                pfold(1)
+                def zall(n):
+                    for f in zstream(n):
+                        f()
+                    if n % 2 == 1:
+                        zdone((n - 13) // 2)
+
+                pfold(0, zrun)
+                pfold(1, zrun)
                 expo(2, D[:, 0])
                 expo(3, D[:, 1])
                 for q in range(XG):
                     load_grad(q + 1)
 
                     def during_t(k):
-                        out = [lambda: zrun(NZT)]
+                        out = []
+                        if q == 3 and k == 8:
+                            out.append(lambda: zall(13))
+                            out.append(lambda: zprep(14))
+                        if q == 3 and k == 12:
+                            out.append(zfold)
                         if 0 < k < 10 and q > 0:
                             g, im = divmod((k - 1) // 2, 2)
                             if k % 2 == 1 and k < 9:
@@ -436,10 +429,15 @@ def tile_sam_pb_v_kernel(tc, logits, x, w3c, b3c, lse, grad_out, out_0, out_1):
                             place(s)
                         if s > 1 and q + 2 < XG:
                             expo(2 * q + 2 + s, D[:, s - 2])
+                        if s == 2 and q in (1, 4):
+                            zall(12 if q == 1 else 14)
+                            zprep(13 if q == 1 else 15)
+                        if s == 3 and q in (1, 4):
+                            zfold()
 
                     def during_m(s):
                         if 0 < s < 3 and q + 1 < XG:
-                            return [lambda: zrun(NZM), lambda: pfold(s - 1)]
+                            return [lambda: zrun(NZM), lambda: pfold(s - 1, zrun)]
                         out = [lambda: zrun(NZM)]
                         if q == 5:
                             for k in (2 * s, 2 * s + 1):
@@ -447,13 +445,11 @@ def tile_sam_pb_v_kernel(tc, logits, x, w3c, b3c, lse, grad_out, out_0, out_1):
                         return out
 
                     mstage(q, before_m, during_m)
-                while todo:
-                    zrun(1000)
+                zall(15)
                 for g in range(2):
                     for im in range(2):
                         dz_split(XG - 1, g, im)
                         dz_round(XG - 1, g, im)
-                zdone(1)
 
         with ExitStack() as ectx:
             fin = ectx.enter_context(tc.tile_pool(name="fin", bufs=2))

from contextlib import ExitStack

import concourse.mybir as mybir
from concourse.masks import make_identity

F32 = mybir.dt.float32
BF16 = mybir.dt.bfloat16
U32 = mybir.dt.uint32
U8 = mybir.dt.uint8
E4X4 = mybir.dt.float8_e4m3fn_x4
E5X4 = mybir.dt.float8_e5m2_x4
ADD = mybir.AluOpType.add
SUB = mybir.AluOpType.subtract
MUL = mybir.AluOpType.mult
EXP = mybir.ActivationFunctionType.Exp
COPY = mybir.ActivationFunctionType.Copy
AX = mybir.AxisListType.X

FLOPS = 2 * 2 * 1024 * 1024 * 1024 + 2 * 49 * 1024 * 1024

PITCH = 129
BASE = 36 * PITCH
PLEN = 16384
XG = 6
NZT = 2
NZM = 5


def tile_sam_pb_v_kernel(tc, logits, x, w3c, b3c, lse, grad_out, out_0, out_1):
    nc = tc.nc
    with ExitStack() as ctx:
        keep = ctx.enter_context(tc.tile_pool(name="keep", bufs=1))
        identf = keep.tile([128, 128], F32, name="identf")
        make_identity(nc, identf[:])
        swapf = keep.tile([128, 128], F32, name="swapf")
        nc.vector.tensor_copy(out=swapf[:, 0:64], in_=identf[:, 64:128])
        nc.vector.tensor_copy(out=swapf[:, 64:128], in_=identf[:, 0:64])
        identb = keep.tile([128, 128], BF16, name="identb")
        make_identity(nc, identb[:])
        par = keep.tile([128, 2], F32, name="par")
        nc.vector.tensor_reduce(par[:], identf[:].rearrange("p (n e) -> p e n", e=2), axis=AX, op=ADD)

        qf = [keep.tile([128, 1024, 4], BF16, name="qf%d" % g, align_bytes=64) for g in range(2)]
        wc = [keep.tile([128, 1024], U32, name="wc%d" % g, align_bytes=64) for g in range(2)]
        ws = [keep.tile([128, 1024], U8, name="ws%d" % g, align_bytes=64) for g in range(2)]
        xc = [keep.tile([128, 1024], U32, name="xc%d" % g, align_bytes=64) for g in range(2)]
        xs = [keep.tile([128, 1024], U8, name="xs%d" % g, align_bytes=64) for g in range(2)]

        qc = [[keep.tile([128, 512], U32, name="qc%d" % g, align_bytes=64)] for g in range(2)]
        qs = [[keep.tile([128, 512], U8, name="qs%d" % g, align_bytes=64)] for g in range(2)]
        tcod = [keep.tile([128, 1024], U32, name="tc0", align_bytes=64)]
        tsc = [keep.tile([128, 1024], U8, name="ts0", align_bytes=64)]
        o0 = out_0.rearrange("b (k c) i j -> k c b (i j)", c=128)
        o1 = out_1.rearrange("(g p t) w -> g t p w", g=2, t=4)

        def code_features(h):
            for g in range(2):
                nc.vector.quantize_mx(
                    out=qc[g][h][:].bitcast(E5X4), scales=qs[g][h][:],
                    in_=qf[g][:, 512 * h:512 * h + 512, :].rearrange("p k t -> p (k t)"))

        qts = {}

        def turn_tokens(h, g, t, ps, tag, store, eng):
            if t == 0:
                qts[(h, g)] = store.tile([128, 4, 128, 4], BF16, name="qt", align_bytes=64, bufs=1 if h == 0 else 2)
            qt = qts[(h, g)]
            tb = ps.tile([128, 4, 128], BF16, name=tag)
            for u in range(4):
                nc.tensor.transpose(tb[:, u, :], qf[g][:, 512 * h + u:512 * h + 512:4, t], identb[:])
            eng(out=qt[:, t], in_=tb[:].rearrange("p u o -> p o u"))

        def code_tokens(h, g):
            cols = slice(512 * g, 512 * g + 512)
            nc.vector.quantize_mx(out=tcod[h][:, cols].bitcast(E5X4), scales=tsc[h][:, cols],
                                  in_=qts[(h, g)][:].rearrange("p t o u -> p (t o u)"))

        def gradient_x(h, k, ps, tag, store, stag, sbufs, eng):
            acc = ps.tile([128, 512], F32, name=tag)
            for g in range(2):
                nc.tensor.matmul_mx(
                    out=acc[:], lhsT=wc[g][:, 128 * k:128 * k + 128].bitcast(E4X4),
                    lhsT_scale=ws[g][:, 128 * k:128 * k + 128],
                    rhs=qc[g][h][:].bitcast(E5X4), rhs_scale=qs[g][h][:], start=(g == 0), stop=(g == 1))
            st = store.tile([128, 512], F32, name=stag, bufs=sbufs)
            eng(out=st[:], in_=acc[:])
            nc.sync.dma_start(out=o0[k][:, 8 * h:8 * h + 8, :], in_=st[:].rearrange("p (b n) -> p b n", n=64))

        def gradient_w(gt, ch, ps, tag, store, stag, sbufs, eng):
            acc = ps.tile([128, 512], F32, name=tag)
            for h in range(2):
                nc.tensor.matmul_mx(
                    out=acc[:], lhsT=tcod[h][:, 128 * gt:128 * gt + 128].bitcast(E5X4),
                    lhsT_scale=tsc[h][:, 128 * gt:128 * gt + 128],
                    rhs=xc[h][:, 512 * ch:512 * ch + 512].bitcast(E4X4),
                    rhs_scale=xs[h][:, 512 * ch:512 * ch + 512], start=(h == 0), stop=(h == 1))
            st = store.tile([128, 512], F32, name=stag, bufs=sbufs)
            eng(out=st[:], in_=acc[:])
            nc.sync.dma_start(out=o1[gt // 4][gt % 4][:, 512 * ch:512 * ch + 512], in_=st[:])

        with ExitStack() as mctx:
            big = mctx.enter_context(tc.tile_pool(name="big", bufs=1))
            pool = mctx.enter_context(tc.tile_pool(name="pool", bufs=2))
            psT = mctx.enter_context(tc.psum_pool(name="psT", bufs=4))
            psM = mctx.enter_context(tc.psum_pool(name="psM", bufs=2))
            psA = mctx.enter_context(tc.psum_pool(name="psA", bufs=2))

            lset = big.tile([128, 16, 64], F32, name="lset")
            P = big.tile([128, PLEN], F32, name="P")
            Pv = P[:, BASE:BASE + 56 * PITCH].rearrange("p (x y w) -> p x y w", x=7, y=8)
            D = big.tile([128, 2, 7, 7, 8, 8], F32, name="D")
            Dz = big.tile([128, 7, 7, 8, 8], F32, name="Dz")

            lgs = {}
            gls = {}
            gzs = {}
            order = [0, 1, 12, 2, 3, 4, 5, 6, 13, 7, 8, 9, 14, 10, 11, 15]
            loaded = [0]

            def load_logits():
                if loaded[0] < 16:
                    n = order[loaded[0]]
                    loaded[0] += 1
                    t = pool.tile([128, 49, 64], BF16, name="lg", bufs=2)
                    nc.sync.dma_start(out=t[:], in_=logits[n])
                    lgs[n] = t
                    if n >= 12:
                        t = pool.tile([128, 8, 64], BF16, name="gz", bufs=1)
                        nc.sync.dma_start(out=t[:].rearrange("p c n -> p (c n)"),
                                          in_=grad_out[n].rearrange("(h c) i j -> h (c i j)", c=8))
                        gzs[n] = t

            def load_grad(q):
                if q < XG:
                    t = pool.tile([128, 2, 8, 8, 8], BF16, name="gl", bufs=1)
                    for im in range(2):
                        nc.sync.dma_start(
                            out=t[:, im].rearrange("p c i j -> p (c i j)"),
                            in_=grad_out[2 * q + im].rearrange("(h c) i j -> h (c i j)", c=8))
                    gls[q] = t

            def expo(n, dst, y0=0, y1=7):
                dv = dst[:, y0:y1].rearrange("p y x i j -> p (y x) (i j)")
                nc.vector.tensor_tensor(
                    out=dv, in0=lgs[n][:, 7 * y0:7 * y1, :],
                    in1=lset[:, n:n + 1, :].to_broadcast([128, 7 * (y1 - y0), 64]), op=SUB)
                nc.scalar.activation(out=dv, in_=dv, func=EXP)
                if y1 == 7:
                    load_logits()

            def rowfold(dst, clear):
                for i in (0, 1, 2, 5, 6, 7):
                    A = dst[:, :, :, i, :]
                    if i < 3:
                        ds, ss, dead = slice(4 - i, 7 - 2 * i), slice(2 - i, None, -1), slice(0, 3 - i)
                    else:
                        ds, ss, dead = slice(14 - 2 * i, 10 - i), slice(6, 10 - i, -1), slice(11 - i, 7)
                    nc.gpsimd.tensor_tensor(out=A[:, ds], in0=A[:, ds], in1=A[:, ss], op=ADD)
                    if clear:
                        nc.gpsimd.memset(A[:, dead], 0.0)

            def colfold(rows, fill):
                for j in (0, 1, 2, 5, 6, 7):
                    A = rows(j)
                    if j < 3:
                        ds, ss = slice(2 * j, j + 3), slice(6, 3 + j, -1)
                    else:
                        ds, ss = slice(j - 3, 2 * j - 7), slice(j - 5, None, -1)
                    nc.vector.tensor_tensor(out=A[:, ds], in0=A[:, ds], in1=A[:, ss], op=ADD)
                    fill(1)

            def place(im, eng=nc.scalar.copy):
                for dx in range(7):
                    dst = Pv[:, 6 - dx, 0:7, 65 * im:65 * im + 64].rearrange("p y (j i) -> p y i j", i=8)
                    src = D[:, im, ::-1, dx]
                    eng(out=dst.rearrange("p y i (a b) -> p y a i b", b=4), in_=src.rearrange("p y i (a b) -> p y a i b", b=4))

            def pfold(im, fill):
                colfold(lambda j: Pv[:, :, 0:7, 65 * im + 8 * j:65 * im + 8 * j + 8], fill)

            def zprep(n):
                expo(n, Dz[:])
                t = pool.tile([128, 8, 8, 8], BF16, name="gzt", bufs=1)
                nc.scalar.copy(out=t[:].rearrange("p i j c -> p (i j) c"), in_=gzs[n][:].rearrange("p c n -> p n c"))
                gzs[n] = t

            def zfold():
                rowfold(Dz, False)
                v = Dz[:].rearrange("p y x i j -> p x y i j")
                for j in (0, 1, 2, 5, 6, 7):
                    A = v[:, :, :, :, j]
                    if j < 3:
                        ds, ss = slice(4 - j, 7 - 2 * j), slice(2 - j, None, -1)
                    else:
                        ds, ss = slice(14 - 2 * j, 10 - j), slice(6, 10 - j, -1)
                    nc.gpsimd.tensor_tensor(out=A[:, ds], in0=A[:, ds], in1=A[:, ss], op=ADD)

            zacc = {}

            def zstream(n):
                zq, im = divmod(n - 12, 2)
                if im == 0:
                    zacc[zq] = pool.tile([128, 2, 8, 8, 8], F32, name="zacc", bufs=1)
                acc = zacc[zq]
                gz = gzs[n]
                offs = [(dy, dx) for dy in range(7) for dx in range(7) if (dy, dx) != (3, 3)]
                tmps = {}

                def rect(d):
                    return max(0, 3 - d), min(8, 11 - d)

                def mul(k):
                    dy, dx = offs[k]
                    i0, i1 = rect(dy)
                    j0, j1 = rect(dx)
                    t = pool.tile([128, 8, 8, 8], F32, name="ztmp", bufs=4)
                    nc.vector.tensor_tensor(
                        out=t[:, 0:i1 - i0, 0:j1 - j0], in0=gz[:, i0:i1, j0:j1],
                        in1=Dz[:, dy, dx, i0:i1, j0:j1].unsqueeze(3).to_broadcast([128, i1 - i0, j1 - j0, 8]), op=MUL)
                    tmps[k] = t

                def add(k):
                    dy, dx = offs[k]
                    i0, i1 = rect(dy)
                    j0, j1 = rect(dx)
                    a = acc[:, im, i0 + dy - 3:i1 + dy - 3, j0 + dx - 3:j1 + dx - 3]
                    nc.vector.tensor_tensor(out=a, in0=a, in1=tmps.pop(k)[:, 0:i1 - i0, 0:j1 - j0], op=ADD)

                def first():
                    nc.vector.tensor_tensor(
                        out=acc[:, im], in0=gz[:],
                        in1=Dz[:, 3, 3].unsqueeze(3).to_broadcast([128, 8, 8, 8]), op=MUL)

                todo = [first, lambda: mul(0), lambda: mul(1)]
                for k in range(48):
                    if k + 2 < 48:
                        todo.append(lambda k=k: mul(k + 2))
                    todo.append(lambda k=k: add(k))
                return todo

            def zdone(zq):
                acc = zacc[zq]
                dzz = pool.tile([128, 4, 256], F32, name="qt", align_bytes=64, bufs=1)
                for t2 in range(2):
                    zb = psA.tile([128, 2, 2, 128], F32, name="aux")
                    for tt in range(2):
                        for ch in range(2):
                            nc.tensor.transpose(
                                zb[:, tt, ch, :],
                                acc[:].rearrange("p m i j c -> p c (m i j)")[:, 4 * ch + 2 * t2 + tt, :], identf[:])
                    nc.scalar.copy(out=dzz[:, 2 * t2:2 * t2 + 2, :].rearrange("p t (h c) -> p t h c", c=2),
                                   in_=zb[:].rearrange("p t c h -> p t h c"))
                for g in range(2):
                    zb = psA.tile([128, 4, 128], F32, name="aux")
                    for t in range(4):
                        nc.tensor.transpose(zb[:, t, :], dzz[:, t, 128 * g:128 * g + 128], identf[:])
                    k0 = 128 * (XG + zq)
                    nc.scalar.copy(out=qf[g][:, k0:k0 + 128, :], in_=zb[:].rearrange("p t n -> p n t"))

            gms = {}

            def gprep(q):
                gl = gls[q]
                gr = pool.tile([128, 4, 2, 8, 8, 2], BF16, name="gr", bufs=1)
                for cl in range(4):
                    nc.scalar.copy(
                        out=gr[:, cl],
                        in_=gl[:].rearrange("p m (a b) i j -> p b a j i m", b=4)[:, cl])
                gt = psA.tile([128, 8, 128], BF16, name="aux")
                grv = gr[:].rearrange("p b a j i m -> p (b a) (j i m)")
                for c in range(8):
                    nc.tensor.transpose(gt[:, c, :], grv[:, c, :], identb[:])
                gx = pool.tile([128, 128, 2, 8], BF16, name="gx", bufs=1)
                for im in range(2):
                    nc.scalar.activation(
                        out=gx[:, :, im, :], in_=gt[:].rearrange("p c r -> p r c"),
                        func=COPY, scale=par[:, im:im + 1])
                gms[q] = gx

            wms = {}

            def tstage(q, extra):
                wx = pool.tile([128, 2, 64, 128], BF16, name="wx", bufs=1)
                for k in range(16):
                    tb = psT.tile([128, 4, 128], F32, name="tb")
                    for a in range(4):
                        i, j = divmod(4 * k + a, 8)
                        s = BASE + PITCH * (27 - (8 * j + i))
                        nc.tensor.transpose(tb[:, a, :], P[:, s:s + 65 * 127 + 1:65], identf[:])
                    hi = wx[:, 0, 4 * k:4 * k + 4, :]
                    nc.scalar.copy(out=hi, in_=tb[:])
                    for f in extra(k):
                        f()
                    nc.vector.tensor_tensor(out=wx[:, 1, 4 * k:4 * k + 4, :], in0=tb[:], in1=hi, op=SUB)
                wms[q] = wx

            dzs = {}

            def mstage(q, before, extra):
                gx = gms[q]
                wxv = wms[q][:].rearrange("p a n r -> p (a n) r")
                dzx = pool.tile([128, 2, 8, 128], F32, name="dzx", bufs=1)
                for s in range(4):
                    before(s)
                    mb = psM.tile([128, 8, 64], F32, name="mb")
                    for r in range(32):
                        nc.tensor.matmul(
                            mb[:, :, 2 * r:2 * r + 2], lhsT=wxv[:, :, 32 * s + r],
                            rhs=gx[:, 32 * s + r].rearrange("p m c -> p (m c)"), start=True, stop=True)
                    nc.scalar.copy(out=dzx[:, s // 2, :, 64 * (s % 2):64 * (s % 2) + 64], in_=mb[:])
                    for f in extra(s):
                        f()
                dzs[q] = dzx

            def dz_split(q, g, im):
                dzx = dzs[q]
                zb = psA.tile([128, 4, 128], F32, name="aux")
                for t in range(4):
                    nc.tensor.matmul(zb[:, t, :], lhsT=dzx[:, g, 4 * im + t, :], rhs=identf[:],
                                     start=True, stop=False, is_transpose=True)
                    nc.tensor.matmul(zb[:, t, :], lhsT=dzx[:, g, 4 * im + t, :], rhs=swapf[:],
                                     start=False, stop=True, is_transpose=True)
                zbs[(q, g, im)] = zb

            zbs = {}

            def dz_round(q, g, im):
                zb = zbs[(q, g, im)]
                k0 = 128 * q + 64 * im
                nc.scalar.copy(out=qf[g][:, k0:k0 + 64, :], in_=zb[:, :, 0:64].rearrange("p t n -> p n t"))

            def wprep(n):
                g, cq = divmod(n, 4)
                wl = pool.tile([128, 4, 256], BF16, name="io", bufs=2)
                cols = slice(256 * cq, 256 * cq + 256)
                nc.sync.dma_start(
                    out=wl[:], in_=w3c.rearrange("(g p j) w -> g p j w", g=2, j=4)[g][:, :, cols])
                wi = pool.tile([128, 256, 4], BF16, name="iq", bufs=2, align_bytes=64)
                nc.scalar.copy(out=wi[:], in_=wl[:].rearrange("p j w -> p w j"))
                nc.vector.quantize_mx(out=wc[g][:, cols].bitcast(E4X4), scales=ws[g][:, cols],
                                      in_=wi[:].rearrange("p w j -> p (w j)"))

            def xprep(n):
                xi = pool.tile([128, 2, 128, 4], BF16, name="iq", bufs=2, align_bytes=64)
                xl = pool.tile([128, 16, 64], BF16, name="io", bufs=2)
                nc.sync.dma_start(
                    out=xl[:], in_=x.rearrange("b (k c) i j -> k c b (i j)", c=128)[n])
                xw = xl[:].rearrange("p b n -> p (b n)").bitcast(F32)
                xb = psA.tile([128, 4, 128], F32, name="aux")
                for hv in range(4):
                    h, v = divmod(hv, 2)
                    nc.tensor.transpose(xb[:, hv, :], xw[:, 256 * h + v:256 * h + 256:2], identf[:])
                for h in range(2):
                    nc.scalar.copy(
                        out=xi[:, h].rearrange("p c u -> p (c u)").bitcast(F32).rearrange("p (c v) -> p c v", v=2),
                        in_=xb[:, 2 * h:2 * h + 2, :].rearrange("p v c -> p c v"))
                    cols = slice(128 * n, 128 * n + 128)
                    nc.vector.quantize_mx(out=xc[h][:, cols].bitcast(E4X4), scales=xs[h][:, cols],
                                          in_=xi[:, h].rearrange("p c u -> p (c u)"))

            load_logits()
            nc.sync.dma_start(out=lset[:], in_=lse.rearrange("b h n -> h b n"))
            load_logits()
            load_grad(0)
            nc.gpsimd.memset(P[:, 0:BASE], 0.0)
            nc.vector.memset(P[:, BASE + 55 * PITCH:PLEN], 0.0)
            nc.vector.memset(Pv[:, :, 7, :], 0.0)
            skip = None
            kept = {mybir.EngineType.PE, mybir.EngineType.Pool, mybir.EngineType.SP}
            with tc.manual_schedule(engines=kept):
                for im in range(2):
                    for y in range(7):
                        expo(im, D[:, im], y, y + 1)
                    rowfold(D[:, im], True)
                place(0)
                place(1, nc.vector.tensor_copy)
                zprep(12)
                zfold()
                def zrun(n):
                    return n

                def zall(n):
                    for f in zstream(n):
                        f()
                    if n % 2 == 1:
                        zdone((n - 13) // 2)

                pfold(0, zrun)
                pfold(1, zrun)
                expo(2, D[:, 0])
                expo(3, D[:, 1])
                for q in range(XG):
                    load_grad(q + 1)

                    def during_t(k):
                        out = []
                        if q == 3 and k == 8:
                            out.append(lambda: zall(13))
                            out.append(lambda: zprep(14))
                        if q == 3 and k == 12:
                            out.append(zfold)
                        if 0 < k < 10 and q > 0:
                            g, im = divmod((k - 1) // 2, 2)
                            if k % 2 == 1 and k < 9:
                                out.append(lambda: dz_split(q - 1, g, im))
                            if k % 2 == 0:
                                out.append(lambda: dz_round(q - 1, g, im))
                        if k in (5, 9) and q + 1 < XG:
                            out.append(lambda: rowfold(D[:, (k - 5) // 4], True))
                        if k == 10:
                            out.append(lambda: gprep(q))
                        if q == 5:
                            if k == 10:
                                out.append(lambda: code_features(0))
                            if k % 5 < 4 and k < 10:
                                out.append(lambda: turn_tokens(0, k // 5, k % 5, psA, "aux", pool, nc.scalar.copy))
                            if k in (4, 9):
                                out.append(lambda: code_tokens(0, k // 5))
                        if k in (12, 13) and q < 4:
                            out.append(lambda: wprep(2 * q + k - 12))
                        if k in (14, 15) and 0 < q < 5:
                            out.append(lambda: xprep(2 * q - 2 + k - 14))
                        return out

                    tstage(q, during_t)

                    def before_m(s):
                        if s < 2 and q + 1 < XG:
                            place(s)
                        if s > 1 and q + 2 < XG:
                            expo(2 * q + 2 + s, D[:, s - 2])
                        if s == 2 and q in (1, 4):
                            zall(12 if q == 1 else 14)
                            zprep(13 if q == 1 else 15)
                        if s == 3 and q in (1, 4):
                            zfold()

                    def during_m(s):
                        if 0 < s < 3 and q + 1 < XG:
                            return [lambda: zrun(NZM), lambda: pfold(s - 1, zrun)]
                        out = [lambda: zrun(NZM)]
                        if q == 5:
                            for k in (2 * s, 2 * s + 1):
                                out.append(lambda k=k: gradient_x(0, k, psA, "aux", pool, "io", 2, nc.scalar.copy))
                        return out

                    mstage(q, before_m, during_m)
                zall(15)
                for g in range(2):
                    for im in range(2):
                        dz_split(XG - 1, g, im)
                        dz_round(XG - 1, g, im)

        with ExitStack() as ectx:
            fin = ectx.enter_context(tc.tile_pool(name="fin", bufs=2))
            ps = ectx.enter_context(tc.psum_pool(name="ps", bufs=4))
            for g in range(2):
                qc[g].append(fin.tile([128, 512], U32, name="qcb%d" % g, align_bytes=64, bufs=1))
                qs[g].append(fin.tile([128, 512], U8, name="qsb%d" % g, align_bytes=64, bufs=1))
            tcod.append(fin.tile([128, 1024], U32, name="tc1", align_bytes=64, bufs=1))
            tsc.append(fin.tile([128, 1024], U8, name="ts1", align_bytes=64, bufs=1))
            engines = [nc.vector.tensor_copy, nc.scalar.copy]
            with tc.manual_schedule():
                code_features(1)
                for g in range(2):
                    for t in range(4):
                        turn_tokens(1, g, t, ps, "tt", fin, engines[t % 2])
                    for k in range(4 * g, 4 * g + 4):
                        gradient_x(1, k, ps, "acc", fin, "st", 8, engines[k % 2])
                    code_tokens(1, g)
                for gt in range(8):
                    for ch in range(2):
                        gradient_w(gt, ch, ps, "acc", fin, "st", 8, engines[ch])
